import numpy as np
import ml_dtypes


def mxq(x, axis, fmt="e4m3"):
    dtype, down = {"e4m3": (ml_dtypes.float8_e4m3fn, 7), "e5m2": (ml_dtypes.float8_e5m2, 14)}[fmt]
    v = np.moveaxis(np.asarray(x, np.float32).astype(ml_dtypes.bfloat16).astype(np.float64), axis, -1)
    blocks = v.reshape(v.shape[:-1] + (-1, 32))
    amax = np.abs(blocks).max(-1, keepdims=True)
    byte = np.maximum(np.where(amax > 0, np.frexp(amax)[1] - 1 + 127, 0) - down, 1)
    scale = np.exp2(byte - 127.0)
    codes = (blocks / scale).astype(np.float32).astype(dtype).astype(np.float64)
    return np.moveaxis((codes * scale).reshape(v.shape), -1, axis)


BF16 = ml_dtypes.bfloat16


def bf(x):
    return np.asarray(x, np.float32).astype(BF16)


def f64(x):
    return np.asarray(x).astype(np.float64)


N, D = 4096, 1024
M = D
PI = 3.1415926


def setup_inputs():
    return {"x1": bf(np.random.standard_normal((N, D)) * 0.125), "x2": bf(np.random.standard_normal((M, D)) * 0.125),
            "length_scales": bf(np.random.standard_normal(D) * 0.1), "period": bf(np.random.standard_normal(1) * 0.1)}


def reference(x1, x2, length_scales, period):
    ls = np.exp(f64(length_scales))
    p = np.exp(f64(period))
    s1 = f64(x1) / ls
    s2 = f64(x2) / ls
    sq1 = np.sum(s1 * s1, axis=1)[:, None]
    sq2 = np.sum(s2 * s2, axis=1)[None, :]
    cross = mxq(s1, 1, "e4m3") @ mxq(s2, 1, "e4m3").T
    dist = np.sqrt(np.maximum(sq1 + sq2 - 2.0 * cross, 0.0))
    return np.exp(-2.0 * np.sin(PI * dist / p) ** 2 / (ls * ls))

@@ -1,0 +1,338 @@
+from contextlib import ExitStack
+
+import concourse.mybir as mybir
+from concourse.masks import make_identity
+
+F32 = mybir.dt.float32
+BF16 = mybir.dt.bfloat16
+I32 = mybir.dt.int32
+U32 = mybir.dt.uint32
+U8 = mybir.dt.uint8
+FP8X4 = mybir.dt.float8_e4m3fn_x4
+ALU = mybir.AluOpType
+ACT = mybir.ActivationFunctionType
+AX = mybir.AxisListType
+
+P = 128
+N1 = 4096
+N2 = 1024
+K = 1024
+FLOPS = 2 * N1 * N2 * K
+
+PI_REF = 3.1415926
+PI = 3.141592653589793
+LOG2E = 1.4426950408889634
+SQRT_HALF = 0.7071067811865476
+LN2_HI = 0.693359375
+LN2_MID = -0.00021219444170128554
+LN2_LO = 1.6465717678215697e-12
+EXP_DEG = 12
+
+NPAIR2 = N2 // 256
+NPAIR1 = N1 // 256
+NPAIR = NPAIR2 + NPAIR1
+
+
+def tile_periodickernel_t_kernel(tc, x1, x2, length_scales, period, out):
+    nc = tc.nc
+    x2v = x2.rearrange("(b p) k -> p b k", p=P)
+    x1v = x1.rearrange("(p b) k -> p b k", p=P)
+    outv = out.rearrange("(p b) j -> p b j", p=P)
+
+    with ExitStack() as ctx:
+        ctx.enter_context(tc.manual_schedule())
+        const = ctx.enter_context(tc.tile_pool(name="const", bufs=1))
+        obuf = ctx.enter_context(tc.tile_pool(name="obuf", bufs=1))
+        xin = ctx.enter_context(tc.tile_pool(name="xin", bufs=3))
+        grp = ctx.enter_context(tc.tile_pool(name="grp", bufs=2))
+        sqp = ctx.enter_context(tc.tile_pool(name="sqp", bufs=2))
+        cod = ctx.enter_context(tc.tile_pool(name="cod", bufs=3))
+        npl = ctx.enter_context(tc.tile_pool(name="npl", bufs=2))
+        p_t = ctx.enter_context(tc.psum_pool(name="p_t", bufs=4))
+        p_m = ctx.enter_context(tc.psum_pool(name="p_m", bufs=3))
+        p_q = ctx.enter_context(tc.psum_pool(name="p_q", bufs=1))
+
+        identf = const.tile([P, P], F32, name="identf")
+        make_identity(nc, identf[:])
+
+        lt_bf = const.tile([P, 4, 2], BF16, name="lt_bf")
+        per_bf = const.tile([P, 1], BF16, name="per_bf")
+        with nc.allow_non_contiguous_dma(reason="1024 length scales, two to a partition and chunk"):
+            nc.sync.dma_start(
+                out=lt_bf[:], in_=length_scales.rearrange("(c p e) -> p c e", c=4, p=P, e=2)
+            )
+            nc.sync.dma_start(out=per_bf[:], in_=period.partition_broadcast(P))
+
+        xs_tiles = {}
+
+        def load(h):
+            xs = xin.tile([P, 4, K], BF16, name="xs")
+            if h < 2:
+                nc.sync.dma_start(out=xs[:], in_=x2v[:, 4 * h : 4 * h + 4, :])
+            else:
+                nc.sync.dma_start(out=xs[:], in_=x1v[:, 4 * (h - 2) : 4 * (h - 2) + 4, :])
+            xs_tiles[h] = xs
+
+        for h in range(3):
+            load(h)
+
+        NE = 9
+        xv = const.tile([P, 16], F32, name="xv")
+        nc.vector.tensor_copy(out=xv[:, 0:8], in_=lt_bf[:].rearrange("p c e -> p (c e)"))
+        nc.vector.tensor_copy(out=xv[:, 8:9], in_=per_bf[:])
+        tf = const.tile([P, 16], F32, name="tf")
+        nc.vector.tensor_scalar(
+            out=tf[:, 0:NE], in0=xv[:, 0:NE], scalar1=-LOG2E, scalar2=-126.0,
+            op0=ALU.mult, op1=ALU.max,
+        )
+        n_i = const.tile([P, 16], I32, name="n_i")
+        nc.vector.tensor_scalar(
+            out=n_i[:, 0:NE], in0=tf[:, 0:NE], scalar1=127.0, scalar2=None, op0=ALU.min
+        )
+        n_f = const.tile([P, 16], F32, name="n_f")
+        nc.vector.tensor_copy(out=n_f[:, 0:NE], in_=n_i[:, 0:NE])
+        p2_i = const.tile([P, 16], I32, name="p2_i")
+        nc.vector.tensor_scalar(
+            out=p2_i[:, 0:NE], in0=n_i[:, 0:NE], scalar1=127.0, scalar2=8388608.0,
+            op0=ALU.add, op1=ALU.mult,
+        )
+        r_a = const.tile([P, 16], F32, name="r_a")
+        r_b = const.tile([P, 16], F32, name="r_b")
+        r_c = const.tile([P, 16], F32, name="r_c")
+        nc.vector.scalar_tensor_tensor(
+            out=r_a[:, 0:NE], in0=n_f[:, 0:NE], scalar=-LN2_HI, in1=xv[:, 0:NE],
+            op0=ALU.mult, op1=ALU.subtract,
+        )
+        nc.vector.scalar_tensor_tensor(
+            out=r_b[:, 0:NE], in0=n_f[:, 0:NE], scalar=-LN2_MID, in1=r_a[:, 0:NE],
+            op0=ALU.mult, op1=ALU.add,
+        )
+        nc.vector.scalar_tensor_tensor(
+            out=r_c[:, 0:NE], in0=n_f[:, 0:NE], scalar=-LN2_LO, in1=r_b[:, 0:NE],
+            op0=ALU.mult, op1=ALU.add,
+        )
+        acc_a = const.tile([P, 16], F32, name="acc_a")
+        acc_b = const.tile([P, 16], F32, name="acc_b")
+        accs = [acc_a, acc_b]
+        fact = [1.0]
+        for d in range(1, EXP_DEG + 1):
+            fact.append(fact[d - 1] * d)
+        nc.vector.tensor_scalar(
+            out=accs[0][:, 0:NE], in0=r_c[:, 0:NE], scalar1=1.0 / fact[EXP_DEG],
+            scalar2=None, op0=ALU.mult,
+        )
+        cur = 0
+        for d in range(EXP_DEG - 1, 0, -1):
+            nc.vector.scalar_tensor_tensor(
+                out=accs[1 - cur][:, 0:NE], in0=accs[cur][:, 0:NE],
+                scalar=1.0 / fact[d], in1=r_c[:, 0:NE], op0=ALU.add, op1=ALU.mult,
+            )
+            cur = 1 - cur
+        ex = const.tile([P, 16], F32, name="ex")
+        nc.vector.scalar_tensor_tensor(
+            out=ex[:, 0:NE], in0=accs[cur][:, 0:NE], scalar=1.0,
+            in1=p2_i[:, 0:NE].bitcast(F32), op0=ALU.add, op1=ALU.mult,
+        )
+        a_sb = ex
+        a_half = const.tile([P, 8], F32, name="a_half")
+        nc.vector.tensor_scalar(
+            out=a_half[:], in0=ex[:, 0:8], scalar1=SQRT_HALF, scalar2=None, op0=ALU.mult
+        )
+        w_sb = const.tile([P, 8], F32, name="w_sb")
+        nc.vector.tensor_tensor(out=w_sb[:], in0=ex[:, 0:8], in1=ex[:, 0:8], op=ALU.mult)
+        sc_sb = const.tile([P, 1], F32, name="sc_sb")
+        nc.vector.scalar_tensor_tensor(
+            out=sc_sb[:], in0=ex[:, 8:9], scalar=-2.0 * (PI_REF / PI) ** 2, in1=ex[:, 8:9],
+            op0=ALU.mult, op1=ALU.mult,
+        )
+
+        c2 = const.tile([P, 2, N2], U32, name="c2", align_bytes=64)
+        s2 = const.tile([P, 2, N2], U8, name="s2", align_bytes=64)
+        h2b = const.tile([P, N2], F32, name="h2b")
+        w2b = const.tile([P, N2], F32, name="w2b")
+        h_j = const.tile([P, 8], F32, name="h_j")
+        h_i = const.tile([P, 32], F32, name="h_i")
+
+        o_tiles = [obuf.tile([P, 2, N2], F32, name="o%d" % u) for u in range(NPAIR1)]
+
+        t_tiles = {}
+        g_tiles = {}
+        q_tiles = {}
+        c_tiles = {}
+        qt_tiles = {}
+
+        def stage_a(t):
+            xsf = xs_tiles[t // 2][:].bitcast(F32)
+            banks = []
+            for g in range(2):
+                tb = p_t.tile([P, 2, 256], F32, name="tb")
+                for u in range(2):
+                    for rb in range(2):
+                        c = 2 * g + u
+                        nc.tensor.transpose(
+                            tb[:, u, P * rb : P * rb + P],
+                            xsf[:, 2 * (t % 2) + rb, P * c : P * c + P],
+                            identf[:],
+                        )
+                banks.append(tb)
+            t_tiles[t] = banks
+
+        def squares(t, g):
+            tbv = t_tiles[t][g][:].bitcast(BF16).rearrange("p u (r e) -> p u e r", e=2)
+            q = q_tiles[t]
+            for u in range(2):
+                for e in range(2):
+                    m = 4 * g + 2 * u + e
+                    nc.scalar.activation(
+                        out=q[:, m, :], in_=tbv[:, u, e, :], func=ACT.Square,
+                        scale=a_half[:, m : m + 1],
+                    )
+
+        def exit_mx(t, g):
+            tbv = t_tiles[t][g][:].bitcast(BF16).rearrange("p u (r e) -> p r u e", e=2)
+            av = (
+                a_sb[:, 4 * g : 4 * g + 4]
+                .rearrange("p (o u e) -> p o u e", o=1, u=2)
+                .to_broadcast([P, 256, 2, 2])
+            )
+            nc.vector.tensor_tensor(
+                out=g_tiles[t][:, g].rearrange("p r (u e) -> p r u e", e=2),
+                in0=tbv, in1=av, op=ALU.mult,
+            )
+
+        def stage_b(t):
+            q_tiles[t] = sqp.tile([P, 8, 256], F32, name="q")
+            g_tiles[t] = grp.tile([P, 2, 256, 4], BF16, name="grouped", align_bytes=64)
+            squares(t, 1)
+            exit_mx(t, 0)
+            exit_mx(t, 1)
+            squares(t, 0)
+
+        def stage_qt(t):
+            qt = p_q.tile([P, 2, P], F32, name="qt")
+            q = q_tiles[t]
+            for rb in range(2):
+                for m in range(8):
+                    nc.tensor.matmul(
+                        qt[:, rb, :], lhsT=q[:, m, P * rb : P * rb + P], rhs=identf[:],
+                        is_transpose=True, start=(m == 0), stop=(m == 7),
+                    )
+            qt_tiles[t] = qt
+
+        def stage_quant(t):
+            gt = g_tiles[t]
+            if t < NPAIR2:
+                for g in range(2):
+                    nc.vector.quantize_mx(
+                        out=c2[:, g, 256 * t : 256 * t + 256].bitcast(FP8X4),
+                        scales=s2[:, g, 256 * t : 256 * t + 256],
+                        in_=gt[:, g].rearrange("p r t -> p (r t)"),
+                    )
+            else:
+                cw = cod.tile([P, 2, 256], U32, name="cw", align_bytes=64)
+                cs = cod.tile([P, 2, 256], U8, name="cs", align_bytes=64)
+                nc.vector.quantize_mx(
+                    out=cw[:].rearrange("p g r -> p (g r)").bitcast(FP8X4),
+                    scales=cs[:].rearrange("p g r -> p (g r)"),
+                    in_=gt[:].rearrange("p g r t -> p (g r t)"),
+                )
+                c_tiles[t] = (cw, cs)
+
+        def stage_reduce(t):
+            if t < NPAIR2:
+                dst = h_j[:, 2 * t : 2 * t + 2]
+            else:
+                dst = h_i[:, 2 * (t - NPAIR2) : 2 * (t - NPAIR2) + 2]
+            nc.vector.tensor_reduce(out=dst, in_=qt_tiles[t][:], axis=AX.X, op=ALU.add)
+
+        def spread(src, dst, permuted):
+            for half in range(2):
+                pw = p_m.tile([P, 4, P], F32, name="acc")
+                for m in range(4):
+                    col = 4 * half + m
+                    nc.tensor.matmul(
+                        pw[:, m, :], lhsT=src[:, col : col + 1].to_broadcast([P, P]),
+                        rhs=identf[:], start=True, stop=True,
+                    )
+                if permuted:
+                    nc.scalar.copy(
+                        out=dst[:, 512 * half : 512 * half + 512].rearrange(
+                            "p (c n e) -> p c n e", c=2, e=2
+                        ),
+                        in_=pw[:].rearrange("p (c e) n -> p c n e", e=2),
+                    )
+                else:
+                    nc.scalar.copy(
+                        out=dst[:, 512 * half : 512 * half + 512],
+                        in_=pw[:].rearrange("p m n -> p (m n)"),
+                    )
+
+        def stage_mx(t):
+            u = t - NPAIR2
+            cw, cs = c_tiles[t]
+            for rb in range(2):
+                for jh in range(2):
+                    acc = p_m.tile([P, 512], F32, name="acc")
+                    for g in range(2):
+                        nc.tensor.matmul_mx(
+                            out=acc[:],
+                            lhsT=cw[:, g, P * rb : P * rb + P].bitcast(FP8X4),
+                            lhsT_scale=cs[:, g, P * rb : P * rb + P],
+                            rhs=c2[:, g, 512 * jh : 512 * jh + 512].bitcast(FP8X4),
+                            rhs_scale=s2[:, g, 512 * jh : 512 * jh + 512],
+                            start=(g == 0), stop=(g == 1),
+                        )
+                    nc.vector.scalar_tensor_tensor(
+                        out=o_tiles[u][:, rb, 512 * jh : 512 * jh + 512], in0=acc[:],
+                        scalar=h_i[:, 2 * u + rb : 2 * u + rb + 1],
+                        in1=h2b[:, 512 * jh : 512 * jh + 512],
+                        op0=ALU.subtract, op1=ALU.subtract,
+                    )
+                nc.gpsimd.tensor_scalar(
+                    out=o_tiles[u][:, rb, :], in0=o_tiles[u][:, rb, :],
+                    scalar1=-1.0e-30, scalar2=-3.0e38, op0=ALU.min, op1=ALU.max,
+                )
+
+        def stage_sqrt(t):
+            ov = o_tiles[t - NPAIR2][:].rearrange("p b j -> p (b j)")
+            nc.scalar.activation(out=ov, in_=ov, func=ACT.Sqrt, scale=sc_sb[:, 0:1])
+
+        for s in range(NPAIR + 5):
+            if 0 <= s - 3 < NPAIR:
+                stage_reduce(s - 3)
+            if s < NPAIR:
+                stage_a(s)
+            if s == 2:
+                spread(w_sb, w2b, True)
+            if s - 3 == NPAIR2 - 1:
+                spread(h_j, h2b, False)
+            if 0 <= s - 1 < NPAIR:
+                stage_b(s - 1)
+            if 0 <= s - 2 < NPAIR:
+                stage_qt(s - 2)
+                stage_quant(s - 2)
+            if NPAIR2 <= s - 3 < NPAIR:
+                stage_mx(s - 3)
+            if NPAIR2 <= s - 4 < NPAIR:
+                stage_sqrt(s - 4)
+            if s % 2 == 1 and (s + 5) // 2 < NPAIR // 2:
+                load((s + 5) // 2)
+
+        for u in range(NPAIR1):
+            ov = o_tiles[u][:].rearrange("p b j -> p (b j)")
+            nt = npl.tile([P, 2 * N2], I32, name="nt")
+            nc.vector.tensor_scalar(out=nt[:], in0=ov, scalar1=0.25, scalar2=None, op0=ALU.add)
+            nc.vector.scalar_tensor_tensor(
+                out=ov, in0=ov, scalar=0.25, in1=nt[:], op0=ALU.add, op1=ALU.subtract
+            )
+            nc.scalar.activation(out=ov, in_=ov, func=ACT.Sin, scale=2.0 * PI)
+
+        for u in range(NPAIR1):
+            nc.vector.scalar_tensor_tensor(
+                out=o_tiles[u][:], in0=o_tiles[u][:], scalar=-1.0,
+                in1=w2b[:].rearrange("p (o j) -> p o j", o=1).to_broadcast([P, 2, N2]),
+                op0=ALU.add, op1=ALU.mult,
+            )
+            ov = o_tiles[u][:].rearrange("p b j -> p (b j)")
+            nc.scalar.activation(out=ov, in_=ov, func=ACT.Exp)
+            nc.sync.dma_start(out=outv[:, 2 * u : 2 * u + 2, :], in_=o_tiles[u][:])

@@ -24,9 +24,8 @@ PI = 3.141592653589793
 LOG2E = 1.4426950408889634
 SQRT_HALF = 0.7071067811865476
 LN2_HI = 0.693359375
-LN2_MID = -0.00021219444170128554
-LN2_LO = 1.6465717678215697e-12
-EXP_DEG = 12
+LN2_LO = -0.00021219444170128554
+EXP_DEG = 10
 
 NPAIR2 = N2 // 256
 NPAIR1 = N1 // 256
@@ -43,14 +42,6 @@ def tile_periodickernel_t_kernel(tc, x1, x2, length_scales, period, out):
         ctx.enter_context(tc.manual_schedule())
         const = ctx.enter_context(tc.tile_pool(name="const", bufs=1))
         obuf = ctx.enter_context(tc.tile_pool(name="obuf", bufs=1))
-        xin = ctx.enter_context(tc.tile_pool(name="xin", bufs=3))
-        grp = ctx.enter_context(tc.tile_pool(name="grp", bufs=2))
-        sqp = ctx.enter_context(tc.tile_pool(name="sqp", bufs=2))
-        cod = ctx.enter_context(tc.tile_pool(name="cod", bufs=3))
-        npl = ctx.enter_context(tc.tile_pool(name="npl", bufs=2))
-        p_t = ctx.enter_context(tc.psum_pool(name="p_t", bufs=4))
-        p_m = ctx.enter_context(tc.psum_pool(name="p_m", bufs=3))
-        p_q = ctx.enter_context(tc.psum_pool(name="p_q", bufs=1))
 
         identf = const.tile([P, P], F32, name="identf")
         make_identity(nc, identf[:])
@@ -63,269 +54,309 @@ def tile_periodickernel_t_kernel(tc, x1, x2, length_scales, period, out):
             )
             nc.sync.dma_start(out=per_bf[:], in_=period.partition_broadcast(P))
 
-        xs_tiles = {}
-
-        def load(h):
-            xs = xin.tile([P, 4, K], BF16, name="xs")
-            if h < 2:
-                nc.sync.dma_start(out=xs[:], in_=x2v[:, 4 * h : 4 * h + 4, :])
-            else:
-                nc.sync.dma_start(out=xs[:], in_=x1v[:, 4 * (h - 2) : 4 * (h - 2) + 4, :])
-            xs_tiles[h] = xs
-
-        for h in range(3):
-            load(h)
-
-        NE = 9
-        xv = const.tile([P, 16], F32, name="xv")
-        nc.vector.tensor_copy(out=xv[:, 0:8], in_=lt_bf[:].rearrange("p c e -> p (c e)"))
-        nc.vector.tensor_copy(out=xv[:, 8:9], in_=per_bf[:])
-        tf = const.tile([P, 16], F32, name="tf")
-        nc.vector.tensor_scalar(
-            out=tf[:, 0:NE], in0=xv[:, 0:NE], scalar1=-LOG2E, scalar2=-126.0,
-            op0=ALU.mult, op1=ALU.max,
-        )
-        n_i = const.tile([P, 16], I32, name="n_i")
-        nc.vector.tensor_scalar(
-            out=n_i[:, 0:NE], in0=tf[:, 0:NE], scalar1=127.0, scalar2=None, op0=ALU.min
-        )
-        n_f = const.tile([P, 16], F32, name="n_f")
-        nc.vector.tensor_copy(out=n_f[:, 0:NE], in_=n_i[:, 0:NE])
-        p2_i = const.tile([P, 16], I32, name="p2_i")
-        nc.vector.tensor_scalar(
-            out=p2_i[:, 0:NE], in0=n_i[:, 0:NE], scalar1=127.0, scalar2=8388608.0,
-            op0=ALU.add, op1=ALU.mult,
-        )
-        r_a = const.tile([P, 16], F32, name="r_a")
-        r_b = const.tile([P, 16], F32, name="r_b")
-        r_c = const.tile([P, 16], F32, name="r_c")
-        nc.vector.scalar_tensor_tensor(
-            out=r_a[:, 0:NE], in0=n_f[:, 0:NE], scalar=-LN2_HI, in1=xv[:, 0:NE],
-            op0=ALU.mult, op1=ALU.subtract,
-        )
-        nc.vector.scalar_tensor_tensor(
-            out=r_b[:, 0:NE], in0=n_f[:, 0:NE], scalar=-LN2_MID, in1=r_a[:, 0:NE],
-            op0=ALU.mult, op1=ALU.add,
-        )
-        nc.vector.scalar_tensor_tensor(
-            out=r_c[:, 0:NE], in0=n_f[:, 0:NE], scalar=-LN2_LO, in1=r_b[:, 0:NE],
-            op0=ALU.mult, op1=ALU.add,
-        )
-        acc_a = const.tile([P, 16], F32, name="acc_a")
-        acc_b = const.tile([P, 16], F32, name="acc_b")
-        accs = [acc_a, acc_b]
-        fact = [1.0]
-        for d in range(1, EXP_DEG + 1):
-            fact.append(fact[d - 1] * d)
-        nc.vector.tensor_scalar(
-            out=accs[0][:, 0:NE], in0=r_c[:, 0:NE], scalar1=1.0 / fact[EXP_DEG],
-            scalar2=None, op0=ALU.mult,
-        )
-        cur = 0
-        for d in range(EXP_DEG - 1, 0, -1):
-            nc.vector.scalar_tensor_tensor(
-                out=accs[1 - cur][:, 0:NE], in0=accs[cur][:, 0:NE],
-                scalar=1.0 / fact[d], in1=r_c[:, 0:NE], op0=ALU.add, op1=ALU.mult,
-            )
-            cur = 1 - cur
-        ex = const.tile([P, 16], F32, name="ex")
-        nc.vector.scalar_tensor_tensor(
-            out=ex[:, 0:NE], in0=accs[cur][:, 0:NE], scalar=1.0,
-            in1=p2_i[:, 0:NE].bitcast(F32), op0=ALU.add, op1=ALU.mult,
-        )
-        a_sb = ex
-        a_half = const.tile([P, 8], F32, name="a_half")
-        nc.vector.tensor_scalar(
-            out=a_half[:], in0=ex[:, 0:8], scalar1=SQRT_HALF, scalar2=None, op0=ALU.mult
-        )
-        w_sb = const.tile([P, 8], F32, name="w_sb")
-        nc.vector.tensor_tensor(out=w_sb[:], in0=ex[:, 0:8], in1=ex[:, 0:8], op=ALU.mult)
-        sc_sb = const.tile([P, 1], F32, name="sc_sb")
-        nc.vector.scalar_tensor_tensor(
-            out=sc_sb[:], in0=ex[:, 8:9], scalar=-2.0 * (PI_REF / PI) ** 2, in1=ex[:, 8:9],
-            op0=ALU.mult, op1=ALU.mult,
-        )
-
         c2 = const.tile([P, 2, N2], U32, name="c2", align_bytes=64)
         s2 = const.tile([P, 2, N2], U8, name="s2", align_bytes=64)
         h2b = const.tile([P, N2], F32, name="h2b")
         w2b = const.tile([P, N2], F32, name="w2b")
         h_j = const.tile([P, 8], F32, name="h_j")
         h_i = const.tile([P, 32], F32, name="h_i")
-
         o_tiles = [obuf.tile([P, 2, N2], F32, name="o%d" % u) for u in range(NPAIR1)]
 
-        t_tiles = {}
-        g_tiles = {}
-        q_tiles = {}
-        c_tiles = {}
-        qt_tiles = {}
+        with ExitStack() as ph1:
+            xin = ph1.enter_context(tc.tile_pool(name="xin", bufs=3))
+            grp = ph1.enter_context(tc.tile_pool(name="grp", bufs=2))
+            sqp = ph1.enter_context(tc.tile_pool(name="sqp", bufs=2))
+            cod = ph1.enter_context(tc.tile_pool(name="cod", bufs=3))
+            p_t = ph1.enter_context(tc.psum_pool(name="p_t", bufs=4))
+            p_m = ph1.enter_context(tc.psum_pool(name="p_m", bufs=2))
+            p_q = ph1.enter_context(tc.psum_pool(name="p_q", bufs=2))
 
-        def stage_a(t):
-            xsf = xs_tiles[t // 2][:].bitcast(F32)
-            banks = []
-            for g in range(2):
-                tb = p_t.tile([P, 2, 256], F32, name="tb")
-                for u in range(2):
-                    for rb in range(2):
-                        c = 2 * g + u
-                        nc.tensor.transpose(
-                            tb[:, u, P * rb : P * rb + P],
-                            xsf[:, 2 * (t % 2) + rb, P * c : P * c + P],
-                            identf[:],
-                        )
-                banks.append(tb)
-            t_tiles[t] = banks
+            xs_tiles = {}
 
-        def squares(t, g):
-            tbv = t_tiles[t][g][:].bitcast(BF16).rearrange("p u (r e) -> p u e r", e=2)
-            q = q_tiles[t]
-            for u in range(2):
-                for e in range(2):
-                    m = 4 * g + 2 * u + e
-                    nc.scalar.activation(
-                        out=q[:, m, :], in_=tbv[:, u, e, :], func=ACT.Square,
-                        scale=a_half[:, m : m + 1],
-                    )
-
-        def exit_mx(t, g):
-            tbv = t_tiles[t][g][:].bitcast(BF16).rearrange("p u (r e) -> p r u e", e=2)
-            av = (
-                a_sb[:, 4 * g : 4 * g + 4]
-                .rearrange("p (o u e) -> p o u e", o=1, u=2)
-                .to_broadcast([P, 256, 2, 2])
-            )
-            nc.vector.tensor_tensor(
-                out=g_tiles[t][:, g].rearrange("p r (u e) -> p r u e", e=2),
-                in0=tbv, in1=av, op=ALU.mult,
-            )
-
-        def stage_b(t):
-            q_tiles[t] = sqp.tile([P, 8, 256], F32, name="q")
-            g_tiles[t] = grp.tile([P, 2, 256, 4], BF16, name="grouped", align_bytes=64)
-            squares(t, 1)
-            exit_mx(t, 0)
-            exit_mx(t, 1)
-            squares(t, 0)
-
-        def stage_qt(t):
-            qt = p_q.tile([P, 2, P], F32, name="qt")
-            q = q_tiles[t]
-            for rb in range(2):
-                for m in range(8):
-                    nc.tensor.matmul(
-                        qt[:, rb, :], lhsT=q[:, m, P * rb : P * rb + P], rhs=identf[:],
-                        is_transpose=True, start=(m == 0), stop=(m == 7),
-                    )
-            qt_tiles[t] = qt
-
-        def stage_quant(t):
-            gt = g_tiles[t]
-            if t < NPAIR2:
-                for g in range(2):
-                    nc.vector.quantize_mx(
-                        out=c2[:, g, 256 * t : 256 * t + 256].bitcast(FP8X4),
-                        scales=s2[:, g, 256 * t : 256 * t + 256],
-                        in_=gt[:, g].rearrange("p r t -> p (r t)"),
-                    )
-            else:
-                cw = cod.tile([P, 2, 256], U32, name="cw", align_bytes=64)
-                cs = cod.tile([P, 2, 256], U8, name="cs", align_bytes=64)
-                nc.vector.quantize_mx(
-                    out=cw[:].rearrange("p g r -> p (g r)").bitcast(FP8X4),
-                    scales=cs[:].rearrange("p g r -> p (g r)"),
-                    in_=gt[:].rearrange("p g r t -> p (g r t)"),
-                )
-                c_tiles[t] = (cw, cs)
-
-        def stage_reduce(t):
-            if t < NPAIR2:
-                dst = h_j[:, 2 * t : 2 * t + 2]
-            else:
-                dst = h_i[:, 2 * (t - NPAIR2) : 2 * (t - NPAIR2) + 2]
-            nc.vector.tensor_reduce(out=dst, in_=qt_tiles[t][:], axis=AX.X, op=ALU.add)
-
-        def spread(src, dst, permuted):
-            for half in range(2):
-                pw = p_m.tile([P, 4, P], F32, name="acc")
-                for m in range(4):
-                    col = 4 * half + m
-                    nc.tensor.matmul(
-                        pw[:, m, :], lhsT=src[:, col : col + 1].to_broadcast([P, P]),
-                        rhs=identf[:], start=True, stop=True,
-                    )
-                if permuted:
-                    nc.scalar.copy(
-                        out=dst[:, 512 * half : 512 * half + 512].rearrange(
-                            "p (c n e) -> p c n e", c=2, e=2
-                        ),
-                        in_=pw[:].rearrange("p (c e) n -> p c n e", e=2),
-                    )
+            def load(h):
+                xs = xin.tile([P, 4, K], BF16, name="xs")
+                if h < 2:
+                    nc.sync.dma_start(out=xs[:], in_=x2v[:, 4 * h : 4 * h + 4, :])
                 else:
-                    nc.scalar.copy(
-                        out=dst[:, 512 * half : 512 * half + 512],
-                        in_=pw[:].rearrange("p m n -> p (m n)"),
-                    )
+                    nc.sync.dma_start(out=xs[:], in_=x1v[:, 4 * (h - 2) : 4 * (h - 2) + 4, :])
+                xs_tiles[h] = xs
 
-        def stage_mx(t):
-            u = t - NPAIR2
-            cw, cs = c_tiles[t]
-            for rb in range(2):
-                for jh in range(2):
-                    acc = p_m.tile([P, 512], F32, name="acc")
-                    for g in range(2):
-                        nc.tensor.matmul_mx(
-                            out=acc[:],
-                            lhsT=cw[:, g, P * rb : P * rb + P].bitcast(FP8X4),
-                            lhsT_scale=cs[:, g, P * rb : P * rb + P],
-                            rhs=c2[:, g, 512 * jh : 512 * jh + 512].bitcast(FP8X4),
-                            rhs_scale=s2[:, g, 512 * jh : 512 * jh + 512],
-                            start=(g == 0), stop=(g == 1),
-                        )
-                    nc.vector.scalar_tensor_tensor(
-                        out=o_tiles[u][:, rb, 512 * jh : 512 * jh + 512], in0=acc[:],
-                        scalar=h_i[:, 2 * u + rb : 2 * u + rb + 1],
-                        in1=h2b[:, 512 * jh : 512 * jh + 512],
-                        op0=ALU.subtract, op1=ALU.subtract,
-                    )
-                nc.gpsimd.tensor_scalar(
-                    out=o_tiles[u][:, rb, :], in0=o_tiles[u][:, rb, :],
-                    scalar1=-1.0e-30, scalar2=-3.0e38, op0=ALU.min, op1=ALU.max,
+            for h in range(3):
+                load(h)
+
+            NE = 9
+            xv = const.tile([P, 16], F32, name="xv")
+            nc.vector.tensor_scalar(
+                out=xv[:, 0:8], in0=lt_bf[:].rearrange("p c e -> p (c e)"),
+                scalar1=-87.0, scalar2=87.0, op0=ALU.max, op1=ALU.min,
+            )
+            nc.vector.tensor_scalar(
+                out=xv[:, 8:9], in0=per_bf[:], scalar1=-87.0, scalar2=87.0,
+                op0=ALU.max, op1=ALU.min,
+            )
+            n_i = const.tile([P, 16], I32, name="n_i")
+            nc.vector.tensor_scalar(
+                out=n_i[:, 0:NE], in0=xv[:, 0:NE], scalar1=-LOG2E, scalar2=None, op0=ALU.mult
+            )
+            r_a = const.tile([P, 16], F32, name="r_a")
+            r_b = const.tile([P, 16], F32, name="r_b")
+            nc.vector.scalar_tensor_tensor(
+                out=r_a[:, 0:NE], in0=n_i[:, 0:NE], scalar=-LN2_HI, in1=xv[:, 0:NE],
+                op0=ALU.mult, op1=ALU.subtract,
+            )
+            nc.vector.scalar_tensor_tensor(
+                out=r_b[:, 0:NE], in0=n_i[:, 0:NE], scalar=-LN2_LO, in1=r_a[:, 0:NE],
+                op0=ALU.mult, op1=ALU.add,
+            )
+            p2_i = const.tile([P, 16], I32, name="p2_i")
+            nc.vector.tensor_scalar(
+                out=p2_i[:, 0:NE], in0=n_i[:, 0:NE], scalar1=127.0, scalar2=8388608.0,
+                op0=ALU.add, op1=ALU.mult,
+            )
+            acc_a = const.tile([P, 16], F32, name="acc_a")
+            acc_b = const.tile([P, 16], F32, name="acc_b")
+            accs = [acc_a, acc_b]
+            fact = [1.0]
+            for d in range(1, EXP_DEG + 1):
+                fact.append(fact[d - 1] * d)
+            nc.vector.tensor_scalar(
+                out=accs[0][:, 0:NE], in0=r_b[:, 0:NE], scalar1=1.0 / fact[EXP_DEG],
+                scalar2=None, op0=ALU.mult,
+            )
+            cur = 0
+            for d in range(EXP_DEG - 1, 0, -1):
+                nc.vector.scalar_tensor_tensor(
+                    out=accs[1 - cur][:, 0:NE], in0=accs[cur][:, 0:NE],
+                    scalar=1.0 / fact[d], in1=r_b[:, 0:NE], op0=ALU.add, op1=ALU.mult,
+                )
+                cur = 1 - cur
+            ex = const.tile([P, 16], F32, name="ex")
+            nc.vector.scalar_tensor_tensor(
+                out=ex[:, 0:NE], in0=accs[cur][:, 0:NE], scalar=1.0,
+                in1=p2_i[:, 0:NE].bitcast(F32), op0=ALU.add, op1=ALU.mult,
+            )
+            a_half = const.tile([P, 8], F32, name="a_half")
+            nc.vector.tensor_scalar(
+                out=a_half[:], in0=ex[:, 0:8], scalar1=SQRT_HALF, scalar2=None, op0=ALU.mult
+            )
+            w_sb = const.tile([P, 8], F32, name="w_sb")
+            sc_sb = const.tile([P, 1], F32, name="sc_sb")
+
+            def late_constants():
+                nc.vector.tensor_tensor(out=w_sb[:], in0=ex[:, 0:8], in1=ex[:, 0:8], op=ALU.mult)
+                nc.vector.scalar_tensor_tensor(
+                    out=sc_sb[:], in0=ex[:, 8:9], scalar=-2.0 * (PI_REF / PI) ** 2,
+                    in1=ex[:, 8:9], op0=ALU.mult, op1=ALU.mult,
                 )
 
-        def stage_sqrt(t):
-            ov = o_tiles[t - NPAIR2][:].rearrange("p b j -> p (b j)")
-            nc.scalar.activation(out=ov, in_=ov, func=ACT.Sqrt, scale=sc_sb[:, 0:1])
+            t_tiles = {}
+            g_tiles = {}
+            q_tiles = {}
+            c_tiles = {}
+            qt_tiles = {}
 
-        for s in range(NPAIR + 5):
-            if 0 <= s - 3 < NPAIR:
-                stage_reduce(s - 3)
-            if s < NPAIR:
-                stage_a(s)
-            if s == 2:
-                spread(w_sb, w2b, True)
-            if s - 3 == NPAIR2 - 1:
-                spread(h_j, h2b, False)
-            if 0 <= s - 1 < NPAIR:
-                stage_b(s - 1)
-            if 0 <= s - 2 < NPAIR:
-                stage_qt(s - 2)
-                stage_quant(s - 2)
-            if NPAIR2 <= s - 3 < NPAIR:
-                stage_mx(s - 3)
-            if NPAIR2 <= s - 4 < NPAIR:
-                stage_sqrt(s - 4)
-            if s % 2 == 1 and (s + 5) // 2 < NPAIR // 2:
-                load((s + 5) // 2)
+            def ops_a(t):
+                xsf = xs_tiles[t // 2][:].bitcast(F32)
+                banks = [p_t.tile([P, 2, 256], F32, name="tb") for g in range(2)]
+                t_tiles[t] = banks
+                ops = []
+                for g in range(2):
+                    for u in range(2):
+                        for rb in range(2):
+                            ops.append((banks[g][:, u, P * rb : P * rb + P],
+                                        xsf[:, 2 * (t % 2) + rb, P * (2 * g + u) : P * (2 * g + u) + P],
+                                        True, True))
+                return ops
 
+            def ops_qt(t):
+                qt = p_q.tile([P, 2, P], F32, name="qt")
+                qt_tiles[t] = qt
+                q = q_tiles[t]
+                ops = []
+                for rb in range(2):
+                    for m in range(8):
+                        ops.append((qt[:, rb, :], q[:, m, P * rb : P * rb + P], m == 0, m == 7))
+                return ops
+
+            def run_t(ops):
+                for o_ap, i_ap, first, last in ops:
+                    nc.tensor.matmul(
+                        o_ap, lhsT=i_ap, rhs=identf[:], is_transpose=True, start=first, stop=last
+                    )
+
+            def squares(t, g):
+                tbv = t_tiles[t][g][:].bitcast(BF16).rearrange("p u (r e) -> p u e r", e=2)
+                q = q_tiles[t]
+                for u in range(2):
+                    for e in range(2):
+                        m = 4 * g + 2 * u + e
+                        nc.scalar.activation(
+                            out=q[:, m, :], in_=tbv[:, u, e, :], func=ACT.Square,
+                            scale=a_half[:, m : m + 1],
+                        )
+
+            def exit_mx(t, g):
+                tbv = t_tiles[t][g][:].bitcast(BF16).rearrange("p u (r e) -> p r u e", e=2)
+                av = (
+                    ex[:, 4 * g : 4 * g + 4]
+                    .rearrange("p (o u e) -> p o u e", o=1, u=2)
+                    .to_broadcast([P, 256, 2, 2])
+                )
+                nc.vector.tensor_tensor(
+                    out=g_tiles[t][:, g].rearrange("p r (u e) -> p r u e", e=2),
+                    in0=tbv, in1=av, op=ALU.mult,
+                )
+
+            def quant(t):
+                gt = g_tiles[t]
+                if t < NPAIR2:
+                    for g in range(2):
+                        nc.vector.quantize_mx(
+                            out=c2[:, g, 256 * t : 256 * t + 256].bitcast(FP8X4),
+                            scales=s2[:, g, 256 * t : 256 * t + 256],
+                            in_=gt[:, g].rearrange("p r t -> p (r t)"),
+                        )
+                else:
+                    cw = cod.tile([P, 2, 256], U32, name="cw", align_bytes=64)
+                    cs = cod.tile([P, 2, 256], U8, name="cs", align_bytes=64)
+                    nc.vector.quantize_mx(
+                        out=cw[:].rearrange("p g r -> p (g r)").bitcast(FP8X4),
+                        scales=cs[:].rearrange("p g r -> p (g r)"),
+                        in_=gt[:].rearrange("p g r t -> p (g r t)"),
+                    )
+                    c_tiles[t] = (cw, cs)
+
+            def reduce_h(t):
+                if t < NPAIR2:
+                    dst = h_j[:, 2 * t : 2 * t + 2]
+                else:
+                    dst = h_i[:, 2 * (t - NPAIR2) : 2 * (t - NPAIR2) + 2]
+                nc.vector.tensor_reduce(out=dst, in_=qt_tiles[t][:], axis=AX.X, op=ALU.add)
+
+            def spread(src, dst, permuted):
+                for half in range(2):
+                    pw = p_m.tile([P, 4, P], F32, name="acc")
+                    for m in range(4):
+                        col = 4 * half + m
+                        nc.tensor.matmul(
+                            pw[:, m, :], lhsT=src[:, col : col + 1].to_broadcast([P, P]),
+                            rhs=identf[:], start=True, stop=True,
+                        )
+                    if permuted:
+                        nc.scalar.copy(
+                            out=dst[:, 512 * half : 512 * half + 512].rearrange(
+                                "p (c n e) -> p c n e", c=2, e=2
+                            ),
+                            in_=pw[:].rearrange("p (c e) n -> p c n e", e=2),
+                        )
+                    else:
+                        nc.scalar.copy(
+                            out=dst[:, 512 * half : 512 * half + 512],
+                            in_=pw[:].rearrange("p m n -> p (m n)"),
+                        )
+
+            def mx_bank(t, b):
+                u = t - NPAIR2
+                rb = b // 2
+                jh = b % 2
+                cw, cs = c_tiles[t]
+                acc = p_m.tile([P, 512], F32, name="acc")
+                for g in range(2):
+                    nc.tensor.matmul_mx(
+                        out=acc[:],
+                        lhsT=cw[:, g, P * rb : P * rb + P].bitcast(FP8X4),
+                        lhsT_scale=cs[:, g, P * rb : P * rb + P],
+                        rhs=c2[:, g, 512 * jh : 512 * jh + 512].bitcast(FP8X4),
+                        rhs_scale=s2[:, g, 512 * jh : 512 * jh + 512],
+                        start=(g == 0), stop=(g == 1),
+                    )
+                nc.vector.scalar_tensor_tensor(
+                    out=o_tiles[u][:, rb, 512 * jh : 512 * jh + 512], in0=acc[:],
+                    scalar=h_i[:, 2 * u + rb : 2 * u + rb + 1],
+                    in1=h2b[:, 512 * jh : 512 * jh + 512],
+                    op0=ALU.subtract, op1=ALU.subtract,
+                )
+                if jh == 1:
+                    nc.gpsimd.tensor_scalar(
+                        out=o_tiles[u][:, rb, :], in0=o_tiles[u][:, rb, :],
+                        scalar1=-1.0e-30, scalar2=-3.0e38, op0=ALU.min, op1=ALU.max,
+                    )
+
+            def sqrt_pair(t):
+                ov = o_tiles[t - NPAIR2][:].rearrange("p b j -> p (b j)")
+                nc.scalar.activation(out=ov, in_=ov, func=ACT.Sqrt, scale=sc_sb[:, 0:1])
+
+            for s in range(NPAIR + 5):
+                has_b = 0 <= s - 1 < NPAIR
+                has_c = 0 <= s - 2 < NPAIR
+                has_mx = NPAIR2 <= s - 3 < NPAIR
+                if 0 <= s - 3 < NPAIR:
+                    reduce_h(s - 3)
+                t_ops = []
+                if s < NPAIR:
+                    t_ops.extend(ops_a(s))
+                if has_c:
+                    t_ops.extend(ops_qt(s - 2))
+                if has_b:
+                    q_tiles[s - 1] = sqp.tile([P, 8, 256], F32, name="q")
+                    g_tiles[s - 1] = grp.tile([P, 2, 256, 4], BF16, name="grouped", align_bytes=64)
+                    squares(s - 1, 1)
+                run_t(t_ops[0:6])
+                if s == 2:
+                    late_constants()
+                    spread(w_sb, w2b, True)
+                if s - 3 == NPAIR2 - 1:
+                    spread(h_j, h2b, False)
+                if has_mx:
+                    mx_bank(s - 3, 0)
+                if has_b:
+                    exit_mx(s - 1, 0)
+                run_t(t_ops[6:12])
+                if has_mx:
+                    mx_bank(s - 3, 1)
+                if has_b:
+                    exit_mx(s - 1, 1)
+                    squares(s - 1, 0)
+                run_t(t_ops[12:18])
+                if has_mx:
+                    mx_bank(s - 3, 2)
+                if has_c:
+                    quant(s - 2)
+                run_t(t_ops[18:24])
+                if has_mx:
+                    mx_bank(s - 3, 3)
+                if NPAIR2 <= s - 4 < NPAIR:
+                    sqrt_pair(s - 4)
+                if s % 2 == 1 and (s + 5) // 2 < NPAIR // 2:
+                    load((s + 5) // 2)
+
+        npv = ctx.enter_context(tc.tile_pool(name="npv", bufs=2))
+        nps = ctx.enter_context(tc.tile_pool(name="nps", bufs=2))
+        n_tiles = {}
+
+        def flat(u):
+            return o_tiles[u][:].rearrange("p b j -> p (b j)")
+
+        def round_on_scalar(u):
+            nt = nps.tile([P, 2 * N2], I32, name="nts")
+            nc.scalar.activation(out=nt[:].bitcast(U32), in_=flat(u), func=ACT.Copy, bias=0.25)
+            n_tiles[u] = nt
+
+        round_on_scalar(2)
         for u in range(NPAIR1):
-            ov = o_tiles[u][:].rearrange("p b j -> p (b j)")
-            nt = npl.tile([P, 2 * N2], I32, name="nt")
-            nc.vector.tensor_scalar(out=nt[:], in0=ov, scalar1=0.25, scalar2=None, op0=ALU.add)
+            if u not in n_tiles:
+                nt = npv.tile([P, 2 * N2], I32, name="ntv")
+                nc.vector.tensor_scalar(
+                    out=nt[:], in0=flat(u), scalar1=0.25, scalar2=None, op0=ALU.add
+                )
+                n_tiles[u] = nt
             nc.vector.scalar_tensor_tensor(
-                out=ov, in0=ov, scalar=0.25, in1=nt[:], op0=ALU.add, op1=ALU.subtract
+                out=flat(u), in0=flat(u), scalar=0.25, in1=n_tiles[u][:],
+                op0=ALU.add, op1=ALU.subtract,
             )
-            nc.scalar.activation(out=ov, in_=ov, func=ACT.Sin, scale=2.0 * PI)
+            if u % 3 == 0 and u + 5 < NPAIR1:
+                round_on_scalar(u + 5)
+            nc.scalar.activation(out=flat(u), in_=flat(u), func=ACT.Sin, scale=2.0 * PI)
 
         for u in range(NPAIR1):
             nc.vector.scalar_tensor_tensor(
@@ -333,6 +364,5 @@ def tile_periodickernel_t_kernel(tc, x1, x2, length_scales, period, out):
                 in1=w2b[:].rearrange("p (o j) -> p o j", o=1).to_broadcast([P, 2, N2]),
                 op0=ALU.add, op1=ALU.mult,
             )
-            ov = o_tiles[u][:].rearrange("p b j -> p (b j)")
-            nc.scalar.activation(out=ov, in_=ov, func=ACT.Exp)
+            nc.scalar.activation(out=flat(u), in_=flat(u), func=ACT.Exp)
             nc.sync.dma_start(out=outv[:, 2 * u : 2 * u + 2, :], in_=o_tiles[u][:])

@@ -31,6 +31,14 @@ NPAIR2 = N2 // 256
 NPAIR1 = N1 // 256
 NPAIR = NPAIR2 + NPAIR1
 
+UNIT = 64.0
+BIG = 8388608.0
+NEG_BITS = -889192448.0
+
+
+def on_tensor(u):
+    return u % 4 < 2
+
 
 def tile_periodickernel_t_kernel(tc, x1, x2, length_scales, period, out):
     nc = tc.nc
@@ -45,6 +53,8 @@ def tile_periodickernel_t_kernel(tc, x1, x2, length_scales, period, out):
 
         identf = const.tile([P, P], F32, name="identf")
         make_identity(nc, identf[:])
+        warm = const.tile([P, 1], F32, name="warm")
+        nc.scalar.activation(out=warm[:], in_=identf[:, 0:1], func=ACT.Sqrt)
 
         lt_bf = const.tile([P, 4, 2], BF16, name="lt_bf")
         per_bf = const.tile([P, 1], BF16, name="per_bf")
@@ -60,7 +70,18 @@ def tile_periodickernel_t_kernel(tc, x1, x2, length_scales, period, out):
         w2b = const.tile([P, N2], F32, name="w2b")
         h_j = const.tile([P, 8], F32, name="h_j")
         h_i = const.tile([P, 32], F32, name="h_i")
-        o_tiles = [obuf.tile([P, 2, N2], F32, name="o%d" % u) for u in range(NPAIR1)]
+        o_tiles = []
+        quads = []
+        for u in range(NPAIR1):
+            if on_tensor(u):
+                if u % 4 == 0:
+                    quads.append(obuf.tile([P, 4, N2], F32, name="quad", bufs=NPAIR1 // 4 + 1))
+                o_tiles.append(quads[u // 4][:, 2 * (u % 4) : 2 * (u % 4) + 2, :])
+            else:
+                o_tile = obuf.tile([P, 2, N2], F32, name="o%d" % u)
+                o_tiles.append(o_tile[:])
+        big = const.tile([P, P], F32, name="big")
+        nc.vector.memset(big[:], BIG)
 
         with ExitStack() as ph1:
             xin = ph1.enter_context(tc.tile_pool(name="xin", bufs=3))
@@ -75,8 +96,12 @@ def tile_periodickernel_t_kernel(tc, x1, x2, length_scales, period, out):
 
             def load(h):
                 xs = xin.tile([P, 4, K], BF16, name="xs")
-                if h < 2:
-                    nc.sync.dma_start(out=xs[:], in_=x2v[:, 4 * h : 4 * h + 4, :])
+                if h == 0:
+                    for half in range(2):
+                        blocks = slice(2 * half, 2 * half + 2)
+                        nc.sync.dma_start(out=xs[:, blocks, :], in_=x2v[:, blocks, :])
+                elif h == 1:
+                    nc.sync.dma_start(out=xs[:], in_=x2v[:, 4:8, :])
                 else:
                     nc.sync.dma_start(out=xs[:], in_=x1v[:, 4 * (h - 2) : 4 * (h - 2) + 4, :])
                 xs_tiles[h] = xs
@@ -113,27 +138,43 @@ def tile_periodickernel_t_kernel(tc, x1, x2, length_scales, period, out):
                 out=p2_i[:, 0:NE], in0=n_i[:, 0:NE], scalar1=127.0, scalar2=8388608.0,
                 op0=ALU.add, op1=ALU.mult,
             )
-            acc_a = const.tile([P, 16], F32, name="acc_a")
-            acc_b = const.tile([P, 16], F32, name="acc_b")
-            accs = [acc_a, acc_b]
             fact = [1.0]
             for d in range(1, EXP_DEG + 1):
                 fact.append(fact[d - 1] * d)
+            r_sq = const.tile([P, 16], F32, name="r_sq")
+            nc.vector.tensor_tensor(
+                out=r_sq[:, 0:NE], in0=r_b[:, 0:NE], in1=r_b[:, 0:NE], op=ALU.mult
+            )
+            even_t = [const.tile([P, 16], F32, name="even%d" % i) for i in range(2)]
+            odd_t = [const.tile([P, 16], F32, name="odd%d" % i) for i in range(2)]
             nc.vector.tensor_scalar(
-                out=accs[0][:, 0:NE], in0=r_b[:, 0:NE], scalar1=1.0 / fact[EXP_DEG],
+                out=even_t[0][:, 0:NE], in0=r_sq[:, 0:NE], scalar1=1.0 / fact[EXP_DEG],
+                scalar2=None, op0=ALU.mult,
+            )
+            nc.vector.tensor_scalar(
+                out=odd_t[0][:, 0:NE], in0=r_sq[:, 0:NE], scalar1=1.0 / fact[EXP_DEG - 1],
                 scalar2=None, op0=ALU.mult,
             )
             cur = 0
-            for d in range(EXP_DEG - 1, 0, -1):
+            for d in range(EXP_DEG - 2, 0, -2):
                 nc.vector.scalar_tensor_tensor(
-                    out=accs[1 - cur][:, 0:NE], in0=accs[cur][:, 0:NE],
-                    scalar=1.0 / fact[d], in1=r_b[:, 0:NE], op0=ALU.add, op1=ALU.mult,
+                    out=even_t[1 - cur][:, 0:NE], in0=even_t[cur][:, 0:NE],
+                    scalar=1.0 / fact[d], in1=r_sq[:, 0:NE], op0=ALU.add, op1=ALU.mult,
+                )
+                nc.vector.scalar_tensor_tensor(
+                    out=odd_t[1 - cur][:, 0:NE], in0=odd_t[cur][:, 0:NE],
+                    scalar=1.0 / fact[d - 1],
+                    in1=(r_sq if d > 2 else r_b)[:, 0:NE], op0=ALU.add, op1=ALU.mult,
                 )
                 cur = 1 - cur
-            ex = const.tile([P, 16], F32, name="ex")
+            poly = const.tile([P, 16], F32, name="poly")
             nc.vector.scalar_tensor_tensor(
-                out=ex[:, 0:NE], in0=accs[cur][:, 0:NE], scalar=1.0,
-                in1=p2_i[:, 0:NE].bitcast(F32), op0=ALU.add, op1=ALU.mult,
+                out=poly[:, 0:NE], in0=even_t[cur][:, 0:NE], scalar=1.0,
+                in1=odd_t[cur][:, 0:NE], op0=ALU.add, op1=ALU.add,
+            )
+            ex = const.tile([P, 16], F32, name="ex")
+            nc.vector.tensor_tensor(
+                out=ex[:, 0:NE], in0=poly[:, 0:NE], in1=p2_i[:, 0:NE].bitcast(F32), op=ALU.mult
             )
             a_half = const.tile([P, 8], F32, name="a_half")
             nc.vector.tensor_scalar(
@@ -141,12 +182,16 @@ def tile_periodickernel_t_kernel(tc, x1, x2, length_scales, period, out):
             )
             w_sb = const.tile([P, 8], F32, name="w_sb")
             sc_sb = const.tile([P, 1], F32, name="sc_sb")
+            scu_sb = const.tile([P, 1], F32, name="scu_sb")
 
             def late_constants():
                 nc.vector.tensor_tensor(out=w_sb[:], in0=ex[:, 0:8], in1=ex[:, 0:8], op=ALU.mult)
                 nc.vector.scalar_tensor_tensor(
                     out=sc_sb[:], in0=ex[:, 8:9], scalar=-2.0 * (PI_REF / PI) ** 2,
                     in1=ex[:, 8:9], op0=ALU.mult, op1=ALU.mult,
+                )
+                nc.vector.tensor_scalar(
+                    out=scu_sb[:], in0=sc_sb[:], scalar1=UNIT * UNIT, scalar2=None, op0=ALU.mult
                 )
 
             t_tiles = {}
@@ -233,14 +278,14 @@ def tile_periodickernel_t_kernel(tc, x1, x2, length_scales, period, out):
                     dst = h_i[:, 2 * (t - NPAIR2) : 2 * (t - NPAIR2) + 2]
                 nc.vector.tensor_reduce(out=dst, in_=qt_tiles[t][:], axis=AX.X, op=ALU.add)
 
-            def spread(src, dst, permuted):
+            def spread(src, dst, permuted, pool, tag):
                 for half in range(2):
-                    pw = p_m.tile([P, 4, P], F32, name="acc")
+                    pw = pool.tile([P, 4, P], F32, name=tag)
                     for m in range(4):
                         col = 4 * half + m
                         nc.tensor.matmul(
                             pw[:, m, :], lhsT=src[:, col : col + 1].to_broadcast([P, P]),
-                            rhs=identf[:], start=True, stop=True,
+                            rhs=identf[:], is_transpose=True, start=True, stop=True,
                         )
                     if permuted:
                         nc.scalar.copy(
@@ -277,21 +322,22 @@ def tile_periodickernel_t_kernel(tc, x1, x2, length_scales, period, out):
                     op0=ALU.subtract, op1=ALU.subtract,
                 )
                 if jh == 1:
-                    nc.gpsimd.tensor_scalar(
+                    (nc.vector if t == NPAIR - 1 else nc.gpsimd).tensor_scalar(
                         out=o_tiles[u][:, rb, :], in0=o_tiles[u][:, rb, :],
                         scalar1=-1.0e-30, scalar2=-3.0e38, op0=ALU.min, op1=ALU.max,
                     )
+                    if t == NPAIR - 1:
+                        sqrt_rows(u, slice(rb, rb + 1))
 
-            def sqrt_pair(t):
-                ov = o_tiles[t - NPAIR2][:].rearrange("p b j -> p (b j)")
-                nc.scalar.activation(out=ov, in_=ov, func=ACT.Sqrt, scale=sc_sb[:, 0:1])
+            def sqrt_rows(u, blocks):
+                ov = o_tiles[u][:, blocks, :].rearrange("p b j -> p (b j)")
+                sc = scu_sb if on_tensor(u) else sc_sb
+                nc.scalar.activation(out=ov, in_=ov, func=ACT.Sqrt, scale=sc[:, 0:1])
 
             for s in range(NPAIR + 5):
                 has_b = 0 <= s - 1 < NPAIR
                 has_c = 0 <= s - 2 < NPAIR
                 has_mx = NPAIR2 <= s - 3 < NPAIR
-                if 0 <= s - 3 < NPAIR:
-                    reduce_h(s - 3)
                 t_ops = []
                 if s < NPAIR:
                     t_ops.extend(ops_a(s))
@@ -304,9 +350,10 @@ def tile_periodickernel_t_kernel(tc, x1, x2, length_scales, period, out):
                 run_t(t_ops[0:6])
                 if s == 2:
                     late_constants()
-                    spread(w_sb, w2b, True)
                 if s - 3 == NPAIR2 - 1:
-                    spread(h_j, h2b, False)
+                    spread(h_j, h2b, False, p_m, "acc")
+                if s - 3 == NPAIR - 1:
+                    sqrt_rows(s - 4 - NPAIR2, slice(0, 2))
                 if has_mx:
                     mx_bank(s - 3, 0)
                 if has_b:
@@ -325,44 +372,126 @@ def tile_periodickernel_t_kernel(tc, x1, x2, length_scales, period, out):
                 run_t(t_ops[18:24])
                 if has_mx:
                     mx_bank(s - 3, 3)
-                if NPAIR2 <= s - 4 < NPAIR:
-                    sqrt_pair(s - 4)
+                if has_c:
+                    reduce_h(s - 2)
+                if NPAIR2 <= s - 4 < NPAIR - 2:
+                    sqrt_rows(s - 4 - NPAIR2, slice(0, 2))
+                if s == NPAIR + 1:
+                    spread(w_sb, w2b, True, p_t, "tb")
                 if s % 2 == 1 and (s + 5) // 2 < NPAIR // 2:
                     load((s + 5) // 2)
 
         npv = ctx.enter_context(tc.tile_pool(name="npv", bufs=2))
-        nps = ctx.enter_context(tc.tile_pool(name="nps", bufs=2))
+        p_s = ctx.enter_context(tc.psum_pool(name="p_s", bufs=8))
         n_tiles = {}
+        cos_tiles = {}
 
         def flat(u):
-            return o_tiles[u][:].rearrange("p b j -> p (b j)")
+            return o_tiles[u].rearrange("p b j -> p (b j)")
 
-        def round_on_scalar(u):
-            nt = nps.tile([P, 2 * N2], I32, name="nts")
-            nc.scalar.activation(out=nt[:].bitcast(U32), in_=flat(u), func=ACT.Copy, bias=0.25)
-            n_tiles[u] = nt
-
-        round_on_scalar(2)
-        for u in range(NPAIR1):
-            if u not in n_tiles:
-                nt = npv.tile([P, 2 * N2], I32, name="ntv")
+        def turns_bits(k):
+            nt = npv.tile([P, 4, N2], I32, name="ntb")
+            for h in range(2):
                 nc.vector.tensor_scalar(
-                    out=nt[:], in0=flat(u), scalar1=0.25, scalar2=None, op0=ALU.add
+                    out=nt[:, 2 * h : 2 * h + 2, :], in0=quads[k][:, 2 * h : 2 * h + 2, :],
+                    scalar1=0.25 * UNIT, scalar2=NEG_BITS, op0=ALU.add, op1=ALU.add,
                 )
-                n_tiles[u] = nt
+            n_tiles[k] = nt
+
+        def reduce_on_vector(u):
+            nt = npv.tile([P, 2 * N2], I32, name="ntv")
+            nc.vector.tensor_scalar(
+                out=nt[:], in0=flat(u), scalar1=0.25, scalar2=None, op0=ALU.add
+            )
             nc.vector.scalar_tensor_tensor(
-                out=flat(u), in0=flat(u), scalar=0.25, in1=n_tiles[u][:],
+                out=flat(u), in0=flat(u), scalar=0.25, in1=nt[:],
                 op0=ALU.add, op1=ALU.subtract,
             )
-            if u % 3 == 0 and u + 5 < NPAIR1:
-                round_on_scalar(u + 5)
+
+        def cos_tensor(k):
+            ct = obuf.tile([P, 8, 4 * P], F32, name="quad", bufs=NPAIR1 // 4 + 1)
+            nf = n_tiles[k]
+            for jb in range(8):
+                ps = p_s.tile([P, 4, P], F32, name="ps")
+                cols = slice(P * jb, P * jb + P)
+                for rb in range(4):
+                    for i_ap, first, last in (
+                        (nf[:, rb, cols].bitcast(F32), True, False),
+                        (big[:], False, False),
+                        (quads[k][:, rb, cols], False, True),
+                    ):
+                        nc.tensor.matmul(
+                            ps[:, rb, :], lhsT=i_ap, rhs=identf[:],
+                            is_transpose=True, start=first, stop=last,
+                        )
+                nc.scalar.activation(
+                    out=ct[:, jb, :], in_=ps[:].rearrange("p b r -> p (b r)"),
+                    func=ACT.Sin, scale=2.0 * PI / UNIT, bias=0.5 * PI,
+                )
+            cos_tiles[k] = ct
+
+        def cos_scalar(u):
             nc.scalar.activation(out=flat(u), in_=flat(u), func=ACT.Sin, scale=2.0 * PI)
 
-        for u in range(NPAIR1):
+        turns_bits(0)
+        for k in range(NPAIR1 // 4):
+            if k + 1 < NPAIR1 // 4:
+                turns_bits(k + 1)
+            reduce_on_vector(4 * k + 2)
+            reduce_on_vector(4 * k + 3)
+            cos_tensor(k)
+            cos_scalar(4 * k + 2)
+            cos_scalar(4 * k + 3)
+
+        def scale_vector(u):
             nc.vector.scalar_tensor_tensor(
-                out=o_tiles[u][:], in0=o_tiles[u][:], scalar=-1.0,
+                out=o_tiles[u], in0=o_tiles[u], scalar=-1.0,
                 in1=w2b[:].rearrange("p (o j) -> p o j", o=1).to_broadcast([P, 2, N2]),
                 op0=ALU.add, op1=ALU.mult,
             )
-            nc.scalar.activation(out=flat(u), in_=flat(u), func=ACT.Exp)
-            nc.sync.dma_start(out=outv[:, 2 * u : 2 * u + 2, :], in_=o_tiles[u][:])
+
+        def scale_back(k):
+            ct = cos_tiles[k]
+            ot = obuf.tile([P, 4, N2], F32, name="quad", bufs=NPAIR1 // 4 + 1)
+            for rb in range(4):
+                for half in range(2):
+                    ps = p_s.tile([P, 4, P], F32, name="ps")
+                    for m in range(4):
+                        nc.tensor.matmul(
+                            ps[:, m, :], lhsT=ct[:, 4 * half + m, P * rb : P * rb + P],
+                            rhs=identf[:], is_transpose=True, start=True, stop=True,
+                        )
+                    cols = slice(512 * half, 512 * half + 512)
+                    nc.vector.scalar_tensor_tensor(
+                        out=ot[:, rb, cols], in0=ps[:].rearrange("p m r -> p (m r)"),
+                        scalar=-1.0, in1=w2b[:, cols], op0=ALU.add, op1=ALU.mult,
+                    )
+            o_tiles[4 * k] = ot[:, 0:2, :]
+            o_tiles[4 * k + 1] = ot[:, 2:4, :]
+
+        def exp_store(u, pieces):
+            if pieces == 1:
+                nc.scalar.activation(out=flat(u), in_=flat(u), func=ACT.Exp)
+                nc.sync.dma_start(out=outv[:, 2 * u : 2 * u + 2, :], in_=o_tiles[u])
+                return
+            for b in range(2):
+                for c in range(pieces // 2):
+                    width = 2 * N2 // pieces
+                    cols = slice(width * c, width * c + width)
+                    piece = o_tiles[u][:, b, cols]
+                    nc.scalar.activation(out=piece, in_=piece, func=ACT.Exp)
+                    nc.sync.dma_start(out=outv[:, 2 * u + b, cols], in_=piece)
+
+        for k in range(NPAIR1 // 4):
+            scale_vector(4 * k + 2)
+            exp_store(4 * k + 2, 2 if k == 0 else 1)
+            if k == NPAIR1 // 4 - 1:
+                scale_back(k)
+                exp_store(4 * k, 1)
+                exp_store(4 * k + 1, 1)
+            scale_vector(4 * k + 3)
+            exp_store(4 * k + 3, 4 if k == NPAIR1 // 4 - 1 else 1)
+            if k < NPAIR1 // 4 - 1:
+                scale_back(k)
+                exp_store(4 * k, 1)
+                exp_store(4 * k + 1, 1)

@@ -32,7 +32,6 @@ NPAIR1 = N1 // 256
 NPAIR = NPAIR2 + NPAIR1
 
 UNIT = 64.0
-BIG = 8388608.0
 NEG_BITS = -889192448.0
 
 
@@ -80,8 +79,10 @@ def tile_periodickernel_t_kernel(tc, x1, x2, length_scales, period, out):
             else:
                 o_tile = obuf.tile([P, 2, N2], F32, name="o%d" % u)
                 o_tiles.append(o_tile[:])
-        big = const.tile([P, P], F32, name="big")
-        nc.vector.memset(big[:], BIG)
+        big = const.tile([P, 512], BF16, name="big")
+        nc.vector.memset(big[:], 256.0)
+        zero = const.tile([P, 256], BF16, name="zero")
+        nc.vector.memset(zero[:], 0.0)
 
         with ExitStack() as ph1:
             xin = ph1.enter_context(tc.tile_pool(name="xin", bufs=3))
@@ -414,15 +415,19 @@ def tile_periodickernel_t_kernel(tc, x1, x2, length_scales, period, out):
             for jb in range(8):
                 ps = p_s.tile([P, 4, P], F32, name="ps")
                 cols = slice(P * jb, P * jb + P)
+                psf = ps[:].rearrange("p b r -> p (b r)")
+                nc.tensor.matmul(psf, lhsT=big[:, 0:P], rhs=big[:], start=True, stop=False)
+                nc.tensor.matmul(
+                    psf[:, 0:256], lhsT=big[:, 0:P], rhs=zero[:], start=False, stop=False
+                )
                 for rb in range(4):
-                    for i_ap, first, last in (
-                        (nf[:, rb, cols].bitcast(F32), True, False),
-                        (big[:], False, False),
-                        (quads[k][:, rb, cols], False, True),
+                    for i_ap, last in (
+                        (nf[:, rb, cols].bitcast(F32), False),
+                        (quads[k][:, rb, cols], rb == 3),
                     ):
                         nc.tensor.matmul(
                             ps[:, rb, :], lhsT=i_ap, rhs=identf[:],
-                            is_transpose=True, start=first, stop=last,
+                            is_transpose=True, start=False, stop=last,
                         )
                 nc.scalar.activation(
                     out=ct[:, jb, :], in_=ps[:].rearrange("p b r -> p (b r)"),

@@ -90,8 +90,8 @@ def tile_periodickernel_t_kernel(tc, x1, x2, length_scales, period, out):
             sqp = ph1.enter_context(tc.tile_pool(name="sqp", bufs=2))
             cod = ph1.enter_context(tc.tile_pool(name="cod", bufs=3))
             p_t = ph1.enter_context(tc.psum_pool(name="p_t", bufs=4))
-            p_m = ph1.enter_context(tc.psum_pool(name="p_m", bufs=2))
-            p_q = ph1.enter_context(tc.psum_pool(name="p_q", bufs=2))
+            p_m = ph1.enter_context(tc.psum_pool(name="p_m", bufs=3))
+            p_q = ph1.enter_context(tc.psum_pool(name="p_q", bufs=1))
 
             xs_tiles = {}
 
@@ -348,7 +348,6 @@ def tile_periodickernel_t_kernel(tc, x1, x2, length_scales, period, out):
                     q_tiles[s - 1] = sqp.tile([P, 8, 256], F32, name="q")
                     g_tiles[s - 1] = grp.tile([P, 2, 256, 4], BF16, name="grouped", align_bytes=64)
                     squares(s - 1, 1)
-                run_t(t_ops[0:6])
                 if s == 2:
                     late_constants()
                 if s - 3 == NPAIR2 - 1:
@@ -357,26 +356,23 @@ def tile_periodickernel_t_kernel(tc, x1, x2, length_scales, period, out):
                     sqrt_rows(s - 4 - NPAIR2, slice(0, 2))
                 if has_mx:
                     mx_bank(s - 3, 0)
+                    mx_bank(s - 3, 1)
+                run_t(t_ops[0:12])
                 if has_b:
                     exit_mx(s - 1, 0)
-                run_t(t_ops[6:12])
+                if NPAIR2 <= s - 4 < NPAIR - 2:
+                    sqrt_rows(s - 4 - NPAIR2, slice(0, 2))
                 if has_mx:
-                    mx_bank(s - 3, 1)
+                    mx_bank(s - 3, 2)
+                    mx_bank(s - 3, 3)
+                run_t(t_ops[12:24])
+                if has_c:
+                    quant(s - 2)
                 if has_b:
                     exit_mx(s - 1, 1)
                     squares(s - 1, 0)
-                run_t(t_ops[12:18])
-                if has_mx:
-                    mx_bank(s - 3, 2)
-                if has_c:
-                    quant(s - 2)
-                run_t(t_ops[18:24])
-                if has_mx:
-                    mx_bank(s - 3, 3)
                 if has_c:
                     reduce_h(s - 2)
-                if NPAIR2 <= s - 4 < NPAIR - 2:
-                    sqrt_rows(s - 4 - NPAIR2, slice(0, 2))
                 if s == NPAIR + 1:
                     spread(w_sb, w2b, True, p_t, "tb")
                 if s % 2 == 1 and (s + 5) // 2 < NPAIR // 2:
@@ -412,27 +408,30 @@ def tile_periodickernel_t_kernel(tc, x1, x2, length_scales, period, out):
         def cos_tensor(k):
             ct = obuf.tile([P, 8, 4 * P], F32, name="quad", bufs=NPAIR1 // 4 + 1)
             nf = n_tiles[k]
-            for jb in range(8):
-                ps = p_s.tile([P, 4, P], F32, name="ps")
-                cols = slice(P * jb, P * jb + P)
-                psf = ps[:].rearrange("p b r -> p (b r)")
-                nc.tensor.matmul(psf, lhsT=big[:, 0:P], rhs=big[:], start=True, stop=False)
+            for jp in range(4):
+                banks = [p_s.tile([P, 4, P], F32, name="ps") for i in range(2)]
+                for ps in banks:
+                    psf = ps[:].rearrange("p b r -> p (b r)")
+                    nc.tensor.matmul(psf, lhsT=big[:, 0:P], rhs=big[:], start=True, stop=False)
                 nc.tensor.matmul(
                     psf[:, 0:256], lhsT=big[:, 0:P], rhs=zero[:], start=False, stop=False
                 )
-                for rb in range(4):
-                    for i_ap, last in (
-                        (nf[:, rb, cols].bitcast(F32), False),
-                        (quads[k][:, rb, cols], rb == 3),
-                    ):
-                        nc.tensor.matmul(
-                            ps[:, rb, :], lhsT=i_ap, rhs=identf[:],
-                            is_transpose=True, start=False, stop=last,
-                        )
-                nc.scalar.activation(
-                    out=ct[:, jb, :], in_=ps[:].rearrange("p b r -> p (b r)"),
-                    func=ACT.Sin, scale=2.0 * PI / UNIT, bias=0.5 * PI,
-                )
+                for i in range(2):
+                    cols = slice(P * (2 * jp + i), P * (2 * jp + i) + P)
+                    for rb in range(4):
+                        for i_ap, last in (
+                            (nf[:, rb, cols].bitcast(F32), False),
+                            (quads[k][:, rb, cols], rb == 3),
+                        ):
+                            nc.tensor.matmul(
+                                banks[i][:, rb, :], lhsT=i_ap, rhs=identf[:],
+                                is_transpose=True, start=False, stop=last,
+                            )
+                    nc.scalar.activation(
+                        out=ct[:, 2 * jp + i, :],
+                        in_=banks[i][:].rearrange("p b r -> p (b r)"),
+                        func=ACT.Sin, scale=2.0 * PI / UNIT, bias=0.5 * PI,
+                    )
             cos_tiles[k] = ct
 
         def cos_scalar(u):

@@ -81,7 +81,7 @@ def tile_periodickernel_t_kernel(tc, x1, x2, length_scales, period, out):
                 o_tiles.append(o_tile[:])
         big = const.tile([P, 512], BF16, name="big")
         nc.vector.memset(big[:], 256.0)
-        zero = const.tile([P, 256], BF16, name="zero")
+        zero = const.tile([P, 64], F32, name="zero")
         nc.vector.memset(zero[:], 0.0)
 
         with ExitStack() as ph1:
@@ -277,7 +277,12 @@ def tile_periodickernel_t_kernel(tc, x1, x2, length_scales, period, out):
                     dst = h_j[:, 2 * t : 2 * t + 2]
                 else:
                     dst = h_i[:, 2 * (t - NPAIR2) : 2 * (t - NPAIR2) + 2]
-                nc.vector.tensor_reduce(out=dst, in_=qt_tiles[t][:], axis=AX.X, op=ALU.add)
+                qcopy = sqp.tile([P, 2, P], F32, name="qcopy")
+                for rb in range(2):
+                    nc.scalar.activation(
+                        out=qcopy[:, rb, :], in_=qt_tiles[t][:, rb, :], func=ACT.Copy,
+                        accum_out=dst[:, rb : rb + 1],
+                    )
 
             def spread(src, dst, permuted, pool, tag):
                 for half in range(2):
@@ -335,6 +340,14 @@ def tile_periodickernel_t_kernel(tc, x1, x2, length_scales, period, out):
                 sc = scu_sb if on_tensor(u) else sc_sb
                 nc.scalar.activation(out=ov, in_=ov, func=ACT.Sqrt, scale=sc[:, 0:1])
 
+            def keep_warm(count):
+                pw = p_m.tile([P, 4, P], F32, name="acc")
+                for i in range(count):
+                    nc.tensor.matmul(
+                        pw[:, i % 4, :], lhsT=identf[:], rhs=identf[:], start=True, stop=True
+                    )
+
+            keep_warm(5)
             for s in range(NPAIR + 5):
                 has_b = 0 <= s - 1 < NPAIR
                 has_c = 0 <= s - 2 < NPAIR
@@ -357,6 +370,8 @@ def tile_periodickernel_t_kernel(tc, x1, x2, length_scales, period, out):
                 if has_mx:
                     mx_bank(s - 3, 0)
                     mx_bank(s - 3, 1)
+                elif 2 <= s < NPAIR2 + 3:
+                    keep_warm(4)
                 run_t(t_ops[0:12])
                 if has_b:
                     exit_mx(s - 1, 0)
@@ -414,7 +429,7 @@ def tile_periodickernel_t_kernel(tc, x1, x2, length_scales, period, out):
                     psf = ps[:].rearrange("p b r -> p (b r)")
                     nc.tensor.matmul(psf, lhsT=big[:, 0:P], rhs=big[:], start=True, stop=False)
                 nc.tensor.matmul(
-                    psf[:, 0:256], lhsT=big[:, 0:P], rhs=zero[:], start=False, stop=False
+                    psf[:, 0:64], lhsT=identf[:], rhs=zero[:], start=False, stop=False
                 )
                 for i in range(2):
                     cols = slice(P * (2 * jp + i), P * (2 * jp + i) + P)

@@ -83,9 +83,11 @@ def tile_periodickernel_t_kernel(tc, x1, x2, length_scales, period, out):
         nc.vector.memset(big[:], 256.0)
         zero = const.tile([P, 64], F32, name="zero")
         nc.vector.memset(zero[:], 0.0)
+        w_nat = const.tile([P, 8], F32, name="w_nat")
 
+        xin = ctx.enter_context(tc.tile_pool(name="xin", bufs=3))
+        n_tiles = {}
         with ExitStack() as ph1:
-            xin = ph1.enter_context(tc.tile_pool(name="xin", bufs=3))
             grp = ph1.enter_context(tc.tile_pool(name="grp", bufs=2))
             sqp = ph1.enter_context(tc.tile_pool(name="sqp", bufs=2))
             cod = ph1.enter_context(tc.tile_pool(name="cod", bufs=3))
@@ -340,6 +342,14 @@ def tile_periodickernel_t_kernel(tc, x1, x2, length_scales, period, out):
                 sc = scu_sb if on_tensor(u) else sc_sb
                 nc.scalar.activation(out=ov, in_=ov, func=ACT.Sqrt, scale=sc[:, 0:1])
 
+            def first_turns_bits(h):
+                nt = xin.tile([P, 2, N2], I32, name="xs")
+                nc.vector.tensor_scalar(
+                    out=nt[:], in0=quads[0][:, 2 * h : 2 * h + 2, :],
+                    scalar1=0.25 * UNIT, scalar2=NEG_BITS, op0=ALU.add, op1=ALU.add,
+                )
+                n_tiles.setdefault(0, []).append(nt)
+
             def keep_warm(count):
                 pw = p_m.tile([P, 4, P], F32, name="acc")
                 for i in range(count):
@@ -390,28 +400,30 @@ def tile_periodickernel_t_kernel(tc, x1, x2, length_scales, period, out):
                     reduce_h(s - 2)
                 if s == NPAIR + 1:
                     spread(w_sb, w2b, True, p_t, "tb")
+                if s in (NPAIR, NPAIR + 1):
+                    first_turns_bits(s - NPAIR)
                 if s % 2 == 1 and (s + 5) // 2 < NPAIR // 2:
                     load((s + 5) // 2)
 
-        npv = ctx.enter_context(tc.tile_pool(name="npv", bufs=2))
+        npv = ctx.enter_context(tc.tile_pool(name="npv", bufs=4))
         p_s = ctx.enter_context(tc.psum_pool(name="p_s", bufs=8))
-        n_tiles = {}
         cos_tiles = {}
 
         def flat(u):
             return o_tiles[u].rearrange("p b j -> p (b j)")
 
         def turns_bits(k):
-            nt = npv.tile([P, 4, N2], I32, name="ntb")
+            n_tiles[k] = []
             for h in range(2):
+                nt = npv.tile([P, 2, N2], I32, name="ntb")
                 nc.vector.tensor_scalar(
-                    out=nt[:, 2 * h : 2 * h + 2, :], in0=quads[k][:, 2 * h : 2 * h + 2, :],
+                    out=nt[:], in0=quads[k][:, 2 * h : 2 * h + 2, :],
                     scalar1=0.25 * UNIT, scalar2=NEG_BITS, op0=ALU.add, op1=ALU.add,
                 )
-            n_tiles[k] = nt
+                n_tiles[k].append(nt)
 
         def reduce_on_vector(u):
-            nt = npv.tile([P, 2 * N2], I32, name="ntv")
+            nt = xin.tile([P, 2 * N2], I32, name="xs")
             nc.vector.tensor_scalar(
                 out=nt[:], in0=flat(u), scalar1=0.25, scalar2=None, op0=ALU.add
             )
@@ -420,10 +432,14 @@ def tile_periodickernel_t_kernel(tc, x1, x2, length_scales, period, out):
                 op0=ALU.add, op1=ALU.subtract,
             )
 
-        def cos_tensor(k):
-            ct = obuf.tile([P, 8, 4 * P], F32, name="quad", bufs=NPAIR1 // 4 + 1)
+        def cos_tensor(k, half):
+            if half == 0:
+                cos_tiles[k] = obuf.tile(
+                    [P, 8, 4 * P], F32, name="quad", bufs=NPAIR1 // 4 + 1
+                )
+            ct = cos_tiles[k]
             nf = n_tiles[k]
-            for jp in range(4):
+            for jp in (2 * half, 2 * half + 1):
                 banks = [p_s.tile([P, 4, P], F32, name="ps") for i in range(2)]
                 for ps in banks:
                     psf = ps[:].rearrange("p b r -> p (b r)")
@@ -435,7 +451,7 @@ def tile_periodickernel_t_kernel(tc, x1, x2, length_scales, period, out):
                     cols = slice(P * (2 * jp + i), P * (2 * jp + i) + P)
                     for rb in range(4):
                         for i_ap, last in (
-                            (nf[:, rb, cols].bitcast(F32), False),
+                            (nf[rb // 2][:, rb % 2, cols].bitcast(F32), False),
                             (quads[k][:, rb, cols], rb == 3),
                         ):
                             nc.tensor.matmul(
@@ -447,19 +463,34 @@ def tile_periodickernel_t_kernel(tc, x1, x2, length_scales, period, out):
                         in_=banks[i][:].rearrange("p b r -> p (b r)"),
                         func=ACT.Sin, scale=2.0 * PI / UNIT, bias=0.5 * PI,
                     )
-            cos_tiles[k] = ct
 
         def cos_scalar(u):
             nc.scalar.activation(out=flat(u), in_=flat(u), func=ACT.Sin, scale=2.0 * PI)
 
-        turns_bits(0)
+        def turn_w():
+            for half in range(2):
+                ps = p_s.tile([P, 4, P], F32, name="ps")
+                for m in range(4):
+                    cols = slice(P * (4 * half + m), P * (4 * half + m) + P)
+                    nc.tensor.matmul(
+                        ps[:, m, :], lhsT=w2b[:, cols], rhs=identf[:],
+                        is_transpose=True, start=True, stop=True,
+                    )
+                nc.vector.tensor_copy(
+                    out=w_nat[:, 4 * half : 4 * half + 4].rearrange("p (m o) -> p m o", o=1),
+                    in_=ps[:, :, 0:1],
+                )
+
         for k in range(NPAIR1 // 4):
+            reduce_on_vector(4 * k + 2)
             if k + 1 < NPAIR1 // 4:
                 turns_bits(k + 1)
-            reduce_on_vector(4 * k + 2)
             reduce_on_vector(4 * k + 3)
-            cos_tensor(k)
+            cos_tensor(k, 0)
             cos_scalar(4 * k + 2)
+            cos_tensor(k, 1)
+            if k == 0:
+                turn_w()
             cos_scalar(4 * k + 3)
 
         def scale_vector(u):
@@ -469,7 +500,15 @@ def tile_periodickernel_t_kernel(tc, x1, x2, length_scales, period, out):
                 op0=ALU.add, op1=ALU.mult,
             )
 
-        def scale_back(k):
+        def scale_turned(k):
+            ct = cos_tiles[k]
+            for m in range(8):
+                nc.vector.tensor_scalar(
+                    out=ct[:, m, :], in0=ct[:, m, :], scalar1=-1.0, scalar2=w_nat[:, m : m + 1],
+                    op0=ALU.add, op1=ALU.mult,
+                )
+
+        def exp_turned(k, last):
             ct = cos_tiles[k]
             ot = obuf.tile([P, 4, N2], F32, name="quad", bufs=NPAIR1 // 4 + 1)
             for rb in range(4):
@@ -481,12 +520,18 @@ def tile_periodickernel_t_kernel(tc, x1, x2, length_scales, period, out):
                             rhs=identf[:], is_transpose=True, start=True, stop=True,
                         )
                     cols = slice(512 * half, 512 * half + 512)
-                    nc.vector.scalar_tensor_tensor(
-                        out=ot[:, rb, cols], in0=ps[:].rearrange("p m r -> p (m r)"),
-                        scalar=-1.0, in1=w2b[:, cols], op0=ALU.add, op1=ALU.mult,
+                    nc.scalar.activation(
+                        out=ot[:, rb, cols], in_=ps[:].rearrange("p m r -> p (m r)"),
+                        func=ACT.Exp,
                     )
-            o_tiles[4 * k] = ot[:, 0:2, :]
-            o_tiles[4 * k + 1] = ot[:, 2:4, :]
+                    if last and rb == 3:
+                        nc.sync.dma_start(out=outv[:, 8 * k + 3, cols], in_=ot[:, 3, cols])
+                if last and rb < 3:
+                    nc.sync.dma_start(out=outv[:, 8 * k + rb, :], in_=ot[:, rb, :])
+                elif not last and rb % 2 == 1:
+                    nc.sync.dma_start(
+                        out=outv[:, 8 * k + rb - 1 : 8 * k + rb + 1, :], in_=ot[:, rb - 1 : rb + 1, :]
+                    )
 
         def exp_store(u, pieces):
             if pieces == 1:
@@ -502,15 +547,10 @@ def tile_periodickernel_t_kernel(tc, x1, x2, length_scales, period, out):
                     nc.sync.dma_start(out=outv[:, 2 * u + b, cols], in_=piece)
 
         for k in range(NPAIR1 // 4):
+            last = k == NPAIR1 // 4 - 1
             scale_vector(4 * k + 2)
             exp_store(4 * k + 2, 2 if k == 0 else 1)
-            if k == NPAIR1 // 4 - 1:
-                scale_back(k)
-                exp_store(4 * k, 1)
-                exp_store(4 * k + 1, 1)
             scale_vector(4 * k + 3)
-            exp_store(4 * k + 3, 4 if k == NPAIR1 // 4 - 1 else 1)
-            if k < NPAIR1 // 4 - 1:
-                scale_back(k)
-                exp_store(4 * k, 1)
-                exp_store(4 * k + 1, 1)
+            exp_store(4 * k + 3, 1)
+            scale_turned(k)
+            exp_turned(k, last)

@@ -22,9 +22,7 @@ FLOPS = 2 * N1 * N2 * K
 PI_REF = 3.1415926
 PI = 3.141592653589793
 LOG2E = 1.4426950408889634
-SQRT_HALF = 0.7071067811865476
-LN2_HI = 0.693359375
-LN2_LO = -0.00021219444170128554
+LN2 = 0.6931471805599453
 EXP_DEG = 10
 
 NPAIR2 = N2 // 256
@@ -81,9 +79,22 @@ def tile_periodickernel_t_kernel(tc, x1, x2, length_scales, period, out):
                 o_tiles.append(o_tile[:])
         big = const.tile([P, 512], BF16, name="big")
         nc.vector.memset(big[:], 256.0)
-        zero = const.tile([P, 64], F32, name="zero")
+        zero = const.tile([P, 256], BF16, name="zero")
         nc.vector.memset(zero[:], 0.0)
         w_nat = const.tile([P, 8], F32, name="w_nat")
+
+        def spread(src, pool, tag):
+            banks = []
+            for half in range(2):
+                pw = pool.tile([P, 4, P], F32, name=tag)
+                for m in range(4):
+                    col = 4 * half + m
+                    nc.tensor.matmul(
+                        pw[:, m, :], lhsT=src[:, col : col + 1].to_broadcast([P, P]),
+                        rhs=identf[:], is_transpose=True, start=True, stop=True,
+                    )
+                banks.append(pw)
+            return banks
 
         xin = ctx.enter_context(tc.tile_pool(name="xin", bufs=3))
         n_tiles = {}
@@ -124,17 +135,17 @@ def tile_periodickernel_t_kernel(tc, x1, x2, length_scales, period, out):
             )
             n_i = const.tile([P, 16], I32, name="n_i")
             nc.vector.tensor_scalar(
-                out=n_i[:, 0:NE], in0=xv[:, 0:NE], scalar1=-LOG2E, scalar2=None, op0=ALU.mult
+                out=n_i[:, 0:8], in0=lt_bf[:].rearrange("p c e -> p (c e)"),
+                scalar1=-LOG2E, scalar2=-126.0, op0=ALU.mult, op1=ALU.max,
             )
-            r_a = const.tile([P, 16], F32, name="r_a")
+            nc.vector.tensor_scalar(
+                out=n_i[:, 8:9], in0=per_bf[:], scalar1=-LOG2E, scalar2=-126.0,
+                op0=ALU.mult, op1=ALU.max,
+            )
             r_b = const.tile([P, 16], F32, name="r_b")
             nc.vector.scalar_tensor_tensor(
-                out=r_a[:, 0:NE], in0=n_i[:, 0:NE], scalar=-LN2_HI, in1=xv[:, 0:NE],
+                out=r_b[:, 0:NE], in0=n_i[:, 0:NE], scalar=-LN2, in1=xv[:, 0:NE],
                 op0=ALU.mult, op1=ALU.subtract,
-            )
-            nc.vector.scalar_tensor_tensor(
-                out=r_b[:, 0:NE], in0=n_i[:, 0:NE], scalar=-LN2_LO, in1=r_a[:, 0:NE],
-                op0=ALU.mult, op1=ALU.add,
             )
             p2_i = const.tile([P, 16], I32, name="p2_i")
             nc.vector.tensor_scalar(
@@ -178,10 +189,6 @@ def tile_periodickernel_t_kernel(tc, x1, x2, length_scales, period, out):
             ex = const.tile([P, 16], F32, name="ex")
             nc.vector.tensor_tensor(
                 out=ex[:, 0:NE], in0=poly[:, 0:NE], in1=p2_i[:, 0:NE].bitcast(F32), op=ALU.mult
-            )
-            a_half = const.tile([P, 8], F32, name="a_half")
-            nc.vector.tensor_scalar(
-                out=a_half[:], in0=ex[:, 0:8], scalar1=SQRT_HALF, scalar2=None, op0=ALU.mult
             )
             w_sb = const.tile([P, 8], F32, name="w_sb")
             sc_sb = const.tile([P, 1], F32, name="sc_sb")
@@ -240,7 +247,7 @@ def tile_periodickernel_t_kernel(tc, x1, x2, length_scales, period, out):
                         m = 4 * g + 2 * u + e
                         nc.scalar.activation(
                             out=q[:, m, :], in_=tbv[:, u, e, :], func=ACT.Square,
-                            scale=a_half[:, m : m + 1],
+                            scale=ex[:, m : m + 1],
                         )
 
             def exit_mx(t, g):
@@ -282,31 +289,16 @@ def tile_periodickernel_t_kernel(tc, x1, x2, length_scales, period, out):
                 qcopy = sqp.tile([P, 2, P], F32, name="qcopy")
                 for rb in range(2):
                     nc.scalar.activation(
-                        out=qcopy[:, rb, :], in_=qt_tiles[t][:, rb, :], func=ACT.Copy,
+                        out=qcopy[:, rb, :], in_=qt_tiles[t][:, rb, :], func=ACT.Copy, scale=0.5,
                         accum_out=dst[:, rb : rb + 1],
                     )
 
-            def spread(src, dst, permuted, pool, tag):
-                for half in range(2):
-                    pw = pool.tile([P, 4, P], F32, name=tag)
-                    for m in range(4):
-                        col = 4 * half + m
-                        nc.tensor.matmul(
-                            pw[:, m, :], lhsT=src[:, col : col + 1].to_broadcast([P, P]),
-                            rhs=identf[:], is_transpose=True, start=True, stop=True,
-                        )
-                    if permuted:
-                        nc.scalar.copy(
-                            out=dst[:, 512 * half : 512 * half + 512].rearrange(
-                                "p (c n e) -> p c n e", c=2, e=2
-                            ),
-                            in_=pw[:].rearrange("p (c e) n -> p c n e", e=2),
-                        )
-                    else:
-                        nc.scalar.copy(
-                            out=dst[:, 512 * half : 512 * half + 512],
-                            in_=pw[:].rearrange("p m n -> p (m n)"),
-                        )
+
+            def clamp(engine, u, rb):
+                engine.tensor_scalar(
+                    out=o_tiles[u][:, rb, :], in0=o_tiles[u][:, rb, :],
+                    scalar1=-1.0e-30, scalar2=-3.0e38, op0=ALU.min, op1=ALU.max,
+                )
 
             def mx_bank(t, b):
                 u = t - NPAIR2
@@ -329,13 +321,11 @@ def tile_periodickernel_t_kernel(tc, x1, x2, length_scales, period, out):
                     in1=h2b[:, 512 * jh : 512 * jh + 512],
                     op0=ALU.subtract, op1=ALU.subtract,
                 )
-                if jh == 1:
-                    (nc.vector if t == NPAIR - 1 else nc.gpsimd).tensor_scalar(
-                        out=o_tiles[u][:, rb, :], in0=o_tiles[u][:, rb, :],
-                        scalar1=-1.0e-30, scalar2=-3.0e38, op0=ALU.min, op1=ALU.max,
-                    )
-                    if t == NPAIR - 1:
-                        sqrt_rows(u, slice(rb, rb + 1))
+                if t < NPAIR - 1 and jh == 1:
+                    clamp(nc.gpsimd, u, rb)
+                elif t == NPAIR - 1 and b >= 2:
+                    clamp(nc.vector, u, b - 2)
+                    sqrt_rows(u, slice(b - 2, b - 1))
 
             def sqrt_rows(u, blocks):
                 ov = o_tiles[u][:, blocks, :].rearrange("p b j -> p (b j)")
@@ -351,11 +341,29 @@ def tile_periodickernel_t_kernel(tc, x1, x2, length_scales, period, out):
                 n_tiles.setdefault(0, []).append(nt)
 
             def keep_warm(count):
-                pw = p_m.tile([P, 4, P], F32, name="acc")
+                pw = p_m.tile([P, 512], F32, name="acc")
                 for i in range(count):
-                    nc.tensor.matmul(
-                        pw[:, i % 4, :], lhsT=identf[:], rhs=identf[:], start=True, stop=True
+                    nc.tensor.matmul(pw[:], lhsT=big[:, 0:P], rhs=big[:], start=True, stop=True)
+
+            def keep_warm_mx(count, width):
+                pw = p_m.tile([P, 512], F32, name="acc")
+                for i in range(count):
+                    nc.tensor.matmul_mx(
+                        out=pw[:, 0:width],
+                        lhsT=c2[:, 0, 0:P].bitcast(FP8X4), lhsT_scale=s2[:, 0, 0:P],
+                        rhs=c2[:, 0, 0:width].bitcast(FP8X4), rhs_scale=s2[:, 0, 0:width],
+                        start=True, stop=True,
                     )
+
+            def fill_warmth(s, half):
+                if s == 2:
+                    keep_warm(2)
+                elif s == 3 and half == 0:
+                    keep_warm(1)
+                elif s in (3, 4):
+                    keep_warm_mx(3, 256)
+                elif 5 <= s < NPAIR2 + 3:
+                    keep_warm_mx(2, 512)
 
             keep_warm(5)
             for s in range(NPAIR + 5):
@@ -374,14 +382,18 @@ def tile_periodickernel_t_kernel(tc, x1, x2, length_scales, period, out):
                 if s == 2:
                     late_constants()
                 if s - 3 == NPAIR2 - 1:
-                    spread(h_j, h2b, False, p_m, "acc")
+                    for half, pw in enumerate(spread(h_j, p_m, "acc")):
+                        nc.scalar.copy(
+                            out=h2b[:, 512 * half : 512 * half + 512],
+                            in_=pw[:].rearrange("p m n -> p (m n)"),
+                        )
                 if s - 3 == NPAIR - 1:
                     sqrt_rows(s - 4 - NPAIR2, slice(0, 2))
                 if has_mx:
                     mx_bank(s - 3, 0)
                     mx_bank(s - 3, 1)
-                elif 2 <= s < NPAIR2 + 3:
-                    keep_warm(4)
+                else:
+                    fill_warmth(s, 0)
                 run_t(t_ops[0:12])
                 if has_b:
                     exit_mx(s - 1, 0)
@@ -390,6 +402,8 @@ def tile_periodickernel_t_kernel(tc, x1, x2, length_scales, period, out):
                 if has_mx:
                     mx_bank(s - 3, 2)
                     mx_bank(s - 3, 3)
+                else:
+                    fill_warmth(s, 1)
                 run_t(t_ops[12:24])
                 if has_c:
                     quant(s - 2)
@@ -398,8 +412,6 @@ def tile_periodickernel_t_kernel(tc, x1, x2, length_scales, period, out):
                     squares(s - 1, 0)
                 if has_c:
                     reduce_h(s - 2)
-                if s == NPAIR + 1:
-                    spread(w_sb, w2b, True, p_t, "tb")
                 if s in (NPAIR, NPAIR + 1):
                     first_turns_bits(s - NPAIR)
                 if s % 2 == 1 and (s + 5) // 2 < NPAIR // 2:
@@ -412,23 +424,26 @@ def tile_periodickernel_t_kernel(tc, x1, x2, length_scales, period, out):
         def flat(u):
             return o_tiles[u].rearrange("p b j -> p (b j)")
 
-        def turns_bits(k):
-            n_tiles[k] = []
-            for h in range(2):
-                nt = npv.tile([P, 2, N2], I32, name="ntb")
-                nc.vector.tensor_scalar(
-                    out=nt[:], in0=quads[k][:, 2 * h : 2 * h + 2, :],
-                    scalar1=0.25 * UNIT, scalar2=NEG_BITS, op0=ALU.add, op1=ALU.add,
-                )
-                n_tiles[k].append(nt)
+        def turns_bits(k, h):
+            nt = npv.tile([P, 2, N2], I32, name="ntb")
+            nc.vector.tensor_scalar(
+                out=nt[:], in0=quads[k][:, 2 * h : 2 * h + 2, :],
+                scalar1=0.25 * UNIT, scalar2=NEG_BITS, op0=ALU.add, op1=ALU.add,
+            )
+            n_tiles.setdefault(k, []).append(nt)
 
-        def reduce_on_vector(u):
-            nt = xin.tile([P, 2 * N2], I32, name="xs")
+        v_tiles = {}
+
+        def turns(u):
+            nt = npv.tile([P, 2 * N2], I32, name="ntv", bufs=2)
             nc.vector.tensor_scalar(
                 out=nt[:], in0=flat(u), scalar1=0.25, scalar2=None, op0=ALU.add
             )
+            v_tiles[u] = nt
+
+        def subtract_turns(u):
             nc.vector.scalar_tensor_tensor(
-                out=flat(u), in0=flat(u), scalar=0.25, in1=nt[:],
+                out=flat(u), in0=flat(u), scalar=0.25, in1=v_tiles[u][:],
                 op0=ALU.add, op1=ALU.subtract,
             )
 
@@ -445,7 +460,7 @@ def tile_periodickernel_t_kernel(tc, x1, x2, length_scales, period, out):
                     psf = ps[:].rearrange("p b r -> p (b r)")
                     nc.tensor.matmul(psf, lhsT=big[:, 0:P], rhs=big[:], start=True, stop=False)
                 nc.tensor.matmul(
-                    psf[:, 0:64], lhsT=identf[:], rhs=zero[:], start=False, stop=False
+                    psf[:, 0:256], lhsT=big[:, 0:P], rhs=zero[:], start=False, stop=False
                 )
                 for i in range(2):
                     cols = slice(P * (2 * jp + i), P * (2 * jp + i) + P)
@@ -467,6 +482,15 @@ def tile_periodickernel_t_kernel(tc, x1, x2, length_scales, period, out):
         def cos_scalar(u):
             nc.scalar.activation(out=flat(u), in_=flat(u), func=ACT.Sin, scale=2.0 * PI)
 
+        def spread_w():
+            for half, pw in enumerate(spread(w_sb, p_s, "ps")):
+                nc.vector.tensor_copy(
+                    out=w2b[:, 512 * half : 512 * half + 512].rearrange(
+                        "p (c n e) -> p c n e", c=2, e=2
+                    ),
+                    in_=pw[:].rearrange("p (c e) n -> p c n e", e=2),
+                )
+
         def turn_w():
             for half in range(2):
                 ps = p_s.tile([P, 4, P], F32, name="ps")
@@ -482,15 +506,21 @@ def tile_periodickernel_t_kernel(tc, x1, x2, length_scales, period, out):
                 )
 
         for k in range(NPAIR1 // 4):
-            reduce_on_vector(4 * k + 2)
+            turns(4 * k + 2)
             if k + 1 < NPAIR1 // 4:
-                turns_bits(k + 1)
-            reduce_on_vector(4 * k + 3)
+                turns_bits(k + 1, 0)
+            else:
+                turns(4 * k + 3)
+            subtract_turns(4 * k + 2)
+            if k + 1 < NPAIR1 // 4:
+                turns(4 * k + 3)
+                turns_bits(k + 1, 1)
+            subtract_turns(4 * k + 3)
             cos_tensor(k, 0)
+            if k == NPAIR1 // 4 - 1:
+                spread_w()
             cos_scalar(4 * k + 2)
             cos_tensor(k, 1)
-            if k == 0:
-                turn_w()
             cos_scalar(4 * k + 3)
 
         def scale_vector(u):
@@ -549,6 +579,8 @@ def tile_periodickernel_t_kernel(tc, x1, x2, length_scales, period, out):
         for k in range(NPAIR1 // 4):
             last = k == NPAIR1 // 4 - 1
             scale_vector(4 * k + 2)
+            if k == 0:
+                turn_w()
             exp_store(4 * k + 2, 2 if k == 0 else 1)
             scale_vector(4 * k + 3)
             exp_store(4 * k + 3, 1)

@@ -360,10 +360,8 @@ def tile_periodickernel_t_kernel(tc, x1, x2, length_scales, period, out):
                     keep_warm(2)
                 elif s == 3 and half == 0:
                     keep_warm(1)
-                elif s in (3, 4):
+                elif 3 <= s < NPAIR2 + 3:
                     keep_warm_mx(3, 256)
-                elif 5 <= s < NPAIR2 + 3:
-                    keep_warm_mx(2, 512)
 
             keep_warm(5)
             for s in range(NPAIR + 5):
@@ -389,14 +387,14 @@ def tile_periodickernel_t_kernel(tc, x1, x2, length_scales, period, out):
                         )
                 if s - 3 == NPAIR - 1:
                     sqrt_rows(s - 4 - NPAIR2, slice(0, 2))
+                if has_b:
+                    exit_mx(s - 1, 0)
                 if has_mx:
                     mx_bank(s - 3, 0)
                     mx_bank(s - 3, 1)
                 else:
                     fill_warmth(s, 0)
                 run_t(t_ops[0:12])
-                if has_b:
-                    exit_mx(s - 1, 0)
                 if NPAIR2 <= s - 4 < NPAIR - 2:
                     sqrt_rows(s - 4 - NPAIR2, slice(0, 2))
                 if has_mx:
@@ -581,7 +579,7 @@ def tile_periodickernel_t_kernel(tc, x1, x2, length_scales, period, out):
             scale_vector(4 * k + 2)
             if k == 0:
                 turn_w()
-            exp_store(4 * k + 2, 2 if k == 0 else 1)
+            exp_store(4 * k + 2, 4 if k == 0 else 1)
             scale_vector(4 * k + 3)
             exp_store(4 * k + 3, 1)
             scale_turned(k)

@@ -294,10 +294,10 @@ def tile_periodickernel_t_kernel(tc, x1, x2, length_scales, period, out):
                     )
 
 
-            def clamp(engine, u, rb):
+            def clamp(engine, rows):
                 engine.tensor_scalar(
-                    out=o_tiles[u][:, rb, :], in0=o_tiles[u][:, rb, :],
-                    scalar1=-1.0e-30, scalar2=-3.0e38, op0=ALU.min, op1=ALU.max,
+                    out=rows, in0=rows, scalar1=-1.0e-30, scalar2=-3.0e38,
+                    op0=ALU.min, op1=ALU.max,
                 )
 
             def mx_bank(t, b):
@@ -322,10 +322,14 @@ def tile_periodickernel_t_kernel(tc, x1, x2, length_scales, period, out):
                     op0=ALU.subtract, op1=ALU.subtract,
                 )
                 if t < NPAIR - 1 and jh == 1:
-                    clamp(nc.gpsimd, u, rb)
-                elif t == NPAIR - 1 and b >= 2:
-                    clamp(nc.vector, u, b - 2)
-                    sqrt_rows(u, slice(b - 2, b - 1))
+                    clamp(nc.gpsimd, o_tiles[u][:, rb, :])
+                elif t == NPAIR - 1:
+                    for late in ([b - 1] if b > 0 else []) + ([b] if b == 3 else []):
+                        piece = o_tiles[u][:, late // 2, 512 * (late % 2) : 512 * (late % 2) + 512]
+                        clamp(nc.vector, piece)
+                        nc.scalar.activation(
+                            out=piece, in_=piece, func=ACT.Sqrt, scale=sc_sb[:, 0:1]
+                        )
 
             def sqrt_rows(u, blocks):
                 ov = o_tiles[u][:, blocks, :].rearrange("p b j -> p (b j)")
@@ -386,9 +390,11 @@ def tile_periodickernel_t_kernel(tc, x1, x2, length_scales, period, out):
                             in_=pw[:].rearrange("p m n -> p (m n)"),
                         )
                 if s - 3 == NPAIR - 1:
-                    sqrt_rows(s - 4 - NPAIR2, slice(0, 2))
+                    sqrt_rows(s - 4 - NPAIR2, slice(1, 2))
                 if has_b:
                     exit_mx(s - 1, 0)
+                if s == NPAIR + 1:
+                    quant(s - 2)
                 if has_mx:
                     mx_bank(s - 3, 0)
                     mx_bank(s - 3, 1)
@@ -396,20 +402,22 @@ def tile_periodickernel_t_kernel(tc, x1, x2, length_scales, period, out):
                     fill_warmth(s, 0)
                 run_t(t_ops[0:12])
                 if NPAIR2 <= s - 4 < NPAIR - 2:
-                    sqrt_rows(s - 4 - NPAIR2, slice(0, 2))
+                    sqrt_rows(s - 4 - NPAIR2, slice(1, 2))
                 if has_mx:
                     mx_bank(s - 3, 2)
                     mx_bank(s - 3, 3)
                 else:
                     fill_warmth(s, 1)
                 run_t(t_ops[12:24])
-                if has_c:
+                if has_c and s <= NPAIR:
                     quant(s - 2)
                 if has_b:
                     exit_mx(s - 1, 1)
                     squares(s - 1, 0)
                 if has_c:
                     reduce_h(s - 2)
+                if NPAIR2 <= s - 3 < NPAIR - 1:
+                    sqrt_rows(s - 3 - NPAIR2, slice(0, 1))
                 if s in (NPAIR, NPAIR + 1):
                     first_turns_bits(s - NPAIR)
                 if s % 2 == 1 and (s + 5) // 2 < NPAIR // 2:

@@ -401,6 +401,8 @@ def tile_periodickernel_t_kernel(tc, x1, x2, length_scales, period, out):
                 else:
                     fill_warmth(s, 0)
                 run_t(t_ops[0:12])
+                if has_c and s <= NPAIR:
+                    quant(s - 2)
                 if NPAIR2 <= s - 4 < NPAIR - 2:
                     sqrt_rows(s - 4 - NPAIR2, slice(1, 2))
                 if has_mx:
@@ -409,8 +411,6 @@ def tile_periodickernel_t_kernel(tc, x1, x2, length_scales, period, out):
                 else:
                     fill_warmth(s, 1)
                 run_t(t_ops[12:24])
-                if has_c and s <= NPAIR:
-                    quant(s - 2)
                 if has_b:
                     exit_mx(s - 1, 1)
                     squares(s - 1, 0)

from contextlib import ExitStack

import concourse.mybir as mybir
from concourse.masks import make_identity

F32 = mybir.dt.float32
BF16 = mybir.dt.bfloat16
I32 = mybir.dt.int32
U32 = mybir.dt.uint32
U8 = mybir.dt.uint8
FP8X4 = mybir.dt.float8_e4m3fn_x4
ALU = mybir.AluOpType
ACT = mybir.ActivationFunctionType
AX = mybir.AxisListType

P = 128
N1 = 4096
N2 = 1024
K = 1024
FLOPS = 2 * N1 * N2 * K

PI_REF = 3.1415926
PI = 3.141592653589793
LOG2E = 1.4426950408889634
LN2 = 0.6931471805599453
EXP_DEG = 10

NPAIR2 = N2 // 256
NPAIR1 = N1 // 256
NPAIR = NPAIR2 + NPAIR1

UNIT = 64.0
NEG_BITS = -889192448.0


def on_tensor(u):
    return u % 4 < 2


def tile_periodickernel_t_kernel(tc, x1, x2, length_scales, period, out):
    nc = tc.nc
    x2v = x2.rearrange("(b p) k -> p b k", p=P)
    x1v = x1.rearrange("(p b) k -> p b k", p=P)
    outv = out.rearrange("(p b) j -> p b j", p=P)

    with ExitStack() as ctx:
        ctx.enter_context(tc.manual_schedule())
        const = ctx.enter_context(tc.tile_pool(name="const", bufs=1))
        obuf = ctx.enter_context(tc.tile_pool(name="obuf", bufs=1))

        identf = const.tile([P, P], F32, name="identf")
        make_identity(nc, identf[:])
        warm = const.tile([P, 1], F32, name="warm")
        nc.scalar.activation(out=warm[:], in_=identf[:, 0:1], func=ACT.Sqrt)

        lt_bf = const.tile([P, 4, 2], BF16, name="lt_bf")
        per_bf = const.tile([P, 1], BF16, name="per_bf")
        with nc.allow_non_contiguous_dma(reason="1024 length scales, two to a partition and chunk"):
            nc.sync.dma_start(
                out=lt_bf[:], in_=length_scales.rearrange("(c p e) -> p c e", c=4, p=P, e=2)
            )
            nc.sync.dma_start(out=per_bf[:], in_=period.partition_broadcast(P))

        c2 = const.tile([P, 2, N2], U32, name="c2", align_bytes=64)
        s2 = const.tile([P, 2, N2], U8, name="s2", align_bytes=64)
        h2b = const.tile([P, N2], F32, name="h2b")
        w2b = const.tile([P, N2], F32, name="w2b")
        h_j = const.tile([P, 8], F32, name="h_j")
        h_i = const.tile([P, 32], F32, name="h_i")
        o_tiles = []
        quads = []
        for u in range(NPAIR1):
            if on_tensor(u):
                if u % 4 == 0:
                    quads.append(obuf.tile([P, 4, N2], F32, name="quad", bufs=NPAIR1 // 4 + 1))
                o_tiles.append(quads[u // 4][:, 2 * (u % 4) : 2 * (u % 4) + 2, :])
            else:
                o_tile = obuf.tile([P, 2, N2], F32, name="o%d" % u)
                o_tiles.append(o_tile[:])
        big = const.tile([P, 512], BF16, name="big")
        nc.vector.memset(big[:], 256.0)
        zero = const.tile([P, 256], BF16, name="zero")
        nc.vector.memset(zero[:], 0.0)
        w_nat = const.tile([P, 8], F32, name="w_nat")

        def spread(src, pool, tag):
            banks = []
            for half in range(2):
                pw = pool.tile([P, 4, P], F32, name=tag)
                for m in range(4):
                    col = 4 * half + m
                    nc.tensor.matmul(
                        pw[:, m, :], lhsT=src[:, col : col + 1].to_broadcast([P, P]),
                        rhs=identf[:], is_transpose=True, start=True, stop=True,
                    )
                banks.append(pw)
            return banks

        xin = ctx.enter_context(tc.tile_pool(name="xin", bufs=3))
        n_tiles = {}
        with ExitStack() as ph1:
            grp = ph1.enter_context(tc.tile_pool(name="grp", bufs=2))
            sqp = ph1.enter_context(tc.tile_pool(name="sqp", bufs=2))
            cod = ph1.enter_context(tc.tile_pool(name="cod", bufs=3))
            p_t = ph1.enter_context(tc.psum_pool(name="p_t", bufs=4))
            p_m = ph1.enter_context(tc.psum_pool(name="p_m", bufs=3))
            p_q = ph1.enter_context(tc.psum_pool(name="p_q", bufs=1))

            xs_tiles = {}

            def load(h):
                xs = xin.tile([P, 4, K], BF16, name="xs")
                if h == 0:
                    for half in range(2):
                        blocks = slice(2 * half, 2 * half + 2)
                        nc.sync.dma_start(out=xs[:, blocks, :], in_=x2v[:, blocks, :])
                elif h == 1:
                    nc.sync.dma_start(out=xs[:], in_=x2v[:, 4:8, :])
                else:
                    nc.sync.dma_start(out=xs[:], in_=x1v[:, 4 * (h - 2) : 4 * (h - 2) + 4, :])
                xs_tiles[h] = xs

            for h in range(3):
                load(h)

            NE = 9
            xv = const.tile([P, 16], F32, name="xv")
            nc.vector.tensor_scalar(
                out=xv[:, 0:8], in0=lt_bf[:].rearrange("p c e -> p (c e)"),
                scalar1=-87.0, scalar2=87.0, op0=ALU.max, op1=ALU.min,
            )
            nc.vector.tensor_scalar(
                out=xv[:, 8:9], in0=per_bf[:], scalar1=-87.0, scalar2=87.0,
                op0=ALU.max, op1=ALU.min,
            )
            n_i = const.tile([P, 16], I32, name="n_i")
            nc.vector.tensor_scalar(
                out=n_i[:, 0:8], in0=lt_bf[:].rearrange("p c e -> p (c e)"),
                scalar1=-LOG2E, scalar2=-126.0, op0=ALU.mult, op1=ALU.max,
            )
            nc.vector.tensor_scalar(
                out=n_i[:, 8:9], in0=per_bf[:], scalar1=-LOG2E, scalar2=-126.0,
                op0=ALU.mult, op1=ALU.max,
            )
            r_b = const.tile([P, 16], F32, name="r_b")
            nc.vector.scalar_tensor_tensor(
                out=r_b[:, 0:NE], in0=n_i[:, 0:NE], scalar=-LN2, in1=xv[:, 0:NE],
                op0=ALU.mult, op1=ALU.subtract,
            )
            p2_i = const.tile([P, 16], I32, name="p2_i")
            nc.vector.tensor_scalar(
                out=p2_i[:, 0:NE], in0=n_i[:, 0:NE], scalar1=127.0, scalar2=8388608.0,
                op0=ALU.add, op1=ALU.mult,
            )
            fact = [1.0]
            for d in range(1, EXP_DEG + 1):
                fact.append(fact[d - 1] * d)
            r_sq = const.tile([P, 16], F32, name="r_sq")
            nc.vector.tensor_tensor(
                out=r_sq[:, 0:NE], in0=r_b[:, 0:NE], in1=r_b[:, 0:NE], op=ALU.mult
            )
            even_t = [const.tile([P, 16], F32, name="even%d" % i) for i in range(2)]
            odd_t = [const.tile([P, 16], F32, name="odd%d" % i) for i in range(2)]
            nc.vector.tensor_scalar(
                out=even_t[0][:, 0:NE], in0=r_sq[:, 0:NE], scalar1=1.0 / fact[EXP_DEG],
                scalar2=None, op0=ALU.mult,
            )
            nc.vector.tensor_scalar(
                out=odd_t[0][:, 0:NE], in0=r_sq[:, 0:NE], scalar1=1.0 / fact[EXP_DEG - 1],
                scalar2=None, op0=ALU.mult,
            )
            cur = 0
            for d in range(EXP_DEG - 2, 0, -2):
                nc.vector.scalar_tensor_tensor(
                    out=even_t[1 - cur][:, 0:NE], in0=even_t[cur][:, 0:NE],
                    scalar=1.0 / fact[d], in1=r_sq[:, 0:NE], op0=ALU.add, op1=ALU.mult,
                )
                nc.vector.scalar_tensor_tensor(
                    out=odd_t[1 - cur][:, 0:NE], in0=odd_t[cur][:, 0:NE],
                    scalar=1.0 / fact[d - 1],
                    in1=(r_sq if d > 2 else r_b)[:, 0:NE], op0=ALU.add, op1=ALU.mult,
                )
                cur = 1 - cur
            poly = const.tile([P, 16], F32, name="poly")
            nc.vector.scalar_tensor_tensor(
                out=poly[:, 0:NE], in0=even_t[cur][:, 0:NE], scalar=1.0,
                in1=odd_t[cur][:, 0:NE], op0=ALU.add, op1=ALU.add,
            )
            ex = const.tile([P, 16], F32, name="ex")
            nc.vector.tensor_tensor(
                out=ex[:, 0:NE], in0=poly[:, 0:NE], in1=p2_i[:, 0:NE].bitcast(F32), op=ALU.mult
            )
            w_sb = const.tile([P, 8], F32, name="w_sb")
            sc_sb = const.tile([P, 1], F32, name="sc_sb")
            scu_sb = const.tile([P, 1], F32, name="scu_sb")

            def late_constants():
                nc.vector.tensor_tensor(out=w_sb[:], in0=ex[:, 0:8], in1=ex[:, 0:8], op=ALU.mult)
                nc.vector.scalar_tensor_tensor(
                    out=sc_sb[:], in0=ex[:, 8:9], scalar=-2.0 * (PI_REF / PI) ** 2,
                    in1=ex[:, 8:9], op0=ALU.mult, op1=ALU.mult,
                )
                nc.vector.tensor_scalar(
                    out=scu_sb[:], in0=sc_sb[:], scalar1=UNIT * UNIT, scalar2=None, op0=ALU.mult
                )

            t_tiles = {}
            g_tiles = {}
            q_tiles = {}
            c_tiles = {}
            qt_tiles = {}

            def ops_a(t):
                xsf = xs_tiles[t // 2][:].bitcast(F32)
                banks = [p_t.tile([P, 2, 256], F32, name="tb") for g in range(2)]
                t_tiles[t] = banks
                ops = []
                for g in range(2):
                    for u in range(2):
                        for rb in range(2):
                            ops.append((banks[g][:, u, P * rb : P * rb + P],
                                        xsf[:, 2 * (t % 2) + rb, P * (2 * g + u) : P * (2 * g + u) + P],
                                        True, True))
                return ops

            def ops_qt(t):
                qt = p_q.tile([P, 2, P], F32, name="qt")
                qt_tiles[t] = qt
                q = q_tiles[t]
                ops = []
                for rb in range(2):
                    for m in range(8):
                        ops.append((qt[:, rb, :], q[:, m, P * rb : P * rb + P], m == 0, m == 7))
                return ops

            def run_t(ops):
                for o_ap, i_ap, first, last in ops:
                    nc.tensor.matmul(
                        o_ap, lhsT=i_ap, rhs=identf[:], is_transpose=True, start=first, stop=last
                    )

            def squares(t, g):
                tbv = t_tiles[t][g][:].bitcast(BF16).rearrange("p u (r e) -> p u e r", e=2)
                q = q_tiles[t]
                for u in range(2):
                    for e in range(2):
                        m = 4 * g + 2 * u + e
                        nc.scalar.activation(
                            out=q[:, m, :], in_=tbv[:, u, e, :], func=ACT.Square,
                            scale=ex[:, m : m + 1],
                        )

            def exit_mx(t, g):
                tbv = t_tiles[t][g][:].bitcast(BF16).rearrange("p u (r e) -> p r u e", e=2)
                av = (
                    ex[:, 4 * g : 4 * g + 4]
                    .rearrange("p (o u e) -> p o u e", o=1, u=2)
                    .to_broadcast([P, 256, 2, 2])
                )
                nc.vector.tensor_tensor(
                    out=g_tiles[t][:, g].rearrange("p r (u e) -> p r u e", e=2),
                    in0=tbv, in1=av, op=ALU.mult,
                )

            def quant(t):
                gt = g_tiles[t]
                if t < NPAIR2:
                    for g in range(2):
                        nc.vector.quantize_mx(
                            out=c2[:, g, 256 * t : 256 * t + 256].bitcast(FP8X4),
                            scales=s2[:, g, 256 * t : 256 * t + 256],
                            in_=gt[:, g].rearrange("p r t -> p (r t)"),
                        )
                else:
                    cw = cod.tile([P, 2, 256], U32, name="cw", align_bytes=64)
                    cs = cod.tile([P, 2, 256], U8, name="cs", align_bytes=64)
                    nc.vector.quantize_mx(
                        out=cw[:].rearrange("p g r -> p (g r)").bitcast(FP8X4),
                        scales=cs[:].rearrange("p g r -> p (g r)"),
                        in_=gt[:].rearrange("p g r t -> p (g r t)"),
                    )
                    c_tiles[t] = (cw, cs)

            def reduce_h(t):
                if t < NPAIR2:
                    dst = h_j[:, 2 * t : 2 * t + 2]
                else:
                    dst = h_i[:, 2 * (t - NPAIR2) : 2 * (t - NPAIR2) + 2]
                qcopy = sqp.tile([P, 2, P], F32, name="qcopy")
                for rb in range(2):
                    nc.scalar.activation(
                        out=qcopy[:, rb, :], in_=qt_tiles[t][:, rb, :], func=ACT.Copy, scale=0.5,
                        accum_out=dst[:, rb : rb + 1],
                    )


            def clamp(engine, rows):
                engine.tensor_scalar(
                    out=rows, in0=rows, scalar1=-1.0e-30, scalar2=-3.0e38,
                    op0=ALU.min, op1=ALU.max,
                )

            def mx_bank(t, b):
                u = t - NPAIR2
                rb = b // 2
                jh = b % 2
                cw, cs = c_tiles[t]
                acc = p_m.tile([P, 512], F32, name="acc")
                for g in range(2):
                    nc.tensor.matmul_mx(
                        out=acc[:],
                        lhsT=cw[:, g, P * rb : P * rb + P].bitcast(FP8X4),
                        lhsT_scale=cs[:, g, P * rb : P * rb + P],
                        rhs=c2[:, g, 512 * jh : 512 * jh + 512].bitcast(FP8X4),
                        rhs_scale=s2[:, g, 512 * jh : 512 * jh + 512],
                        start=(g == 0), stop=(g == 1),
                    )
                nc.vector.scalar_tensor_tensor(
                    out=o_tiles[u][:, rb, 512 * jh : 512 * jh + 512], in0=acc[:],
                    scalar=h_i[:, 2 * u + rb : 2 * u + rb + 1],
                    in1=h2b[:, 512 * jh : 512 * jh + 512],
                    op0=ALU.subtract, op1=ALU.subtract,
                )
                if t < NPAIR - 1 and jh == 1:
                    clamp(nc.gpsimd, o_tiles[u][:, rb, :])
                elif t == NPAIR - 1:
                    for late in ([b - 1] if b > 0 else []) + ([b] if b == 3 else []):
                        piece = o_tiles[u][:, late // 2, 512 * (late % 2) : 512 * (late % 2) + 512]
                        clamp(nc.vector, piece)
                        nc.scalar.activation(
                            out=piece, in_=piece, func=ACT.Sqrt, scale=sc_sb[:, 0:1]
                        )

            def sqrt_rows(u, blocks):
                ov = o_tiles[u][:, blocks, :].rearrange("p b j -> p (b j)")
                sc = scu_sb if on_tensor(u) else sc_sb
                nc.scalar.activation(out=ov, in_=ov, func=ACT.Sqrt, scale=sc[:, 0:1])

            def first_turns_bits(h):
                nt = xin.tile([P, 2, N2], I32, name="xs")
                nc.vector.tensor_scalar(
                    out=nt[:], in0=quads[0][:, 2 * h : 2 * h + 2, :],
                    scalar1=0.25 * UNIT, scalar2=NEG_BITS, op0=ALU.add, op1=ALU.add,
                )
                n_tiles.setdefault(0, []).append(nt)

            def keep_warm(count):
                pw = p_m.tile([P, 512], F32, name="acc")
                for i in range(count):
                    nc.tensor.matmul(pw[:], lhsT=big[:, 0:P], rhs=big[:], start=True, stop=True)

            def keep_warm_mx(count, width):
                pw = p_m.tile([P, 512], F32, name="acc")
                for i in range(count):
                    nc.tensor.matmul_mx(
                        out=pw[:, 0:width],
                        lhsT=c2[:, 0, 0:P].bitcast(FP8X4), lhsT_scale=s2[:, 0, 0:P],
                        rhs=c2[:, 0, 0:width].bitcast(FP8X4), rhs_scale=s2[:, 0, 0:width],
                        start=True, stop=True,
                    )

            def fill_warmth(s, half):
                if s == 2:
                    keep_warm(2)
                elif s == 3 and half == 0:
                    keep_warm(1)
                elif 3 <= s < NPAIR2 + 3:
                    keep_warm_mx(3, 256)

            keep_warm(5)
            for s in range(NPAIR + 5):
                has_b = 0 <= s - 1 < NPAIR
                has_c = 0 <= s - 2 < NPAIR
                has_mx = NPAIR2 <= s - 3 < NPAIR
                t_ops = []
                if s < NPAIR:
                    t_ops.extend(ops_a(s))
                if has_c:
                    t_ops.extend(ops_qt(s - 2))
                if has_b:
                    q_tiles[s - 1] = sqp.tile([P, 8, 256], F32, name="q")
                    g_tiles[s - 1] = grp.tile([P, 2, 256, 4], BF16, name="grouped", align_bytes=64)
                    squares(s - 1, 1)
                if s == 2:
                    late_constants()
                if s - 3 == NPAIR2 - 1:
                    for half, pw in enumerate(spread(h_j, p_m, "acc")):
                        nc.scalar.copy(
                            out=h2b[:, 512 * half : 512 * half + 512],
                            in_=pw[:].rearrange("p m n -> p (m n)"),
                        )
                if s - 3 == NPAIR - 1:
                    sqrt_rows(s - 4 - NPAIR2, slice(1, 2))
                if has_b:
                    exit_mx(s - 1, 0)
                if s == NPAIR + 1:
                    quant(s - 2)
                if has_mx:
                    mx_bank(s - 3, 0)
                    mx_bank(s - 3, 1)
                else:
                    fill_warmth(s, 0)
                run_t(t_ops[0:12])
                if has_c and s <= NPAIR:
                    quant(s - 2)
                if NPAIR2 <= s - 4 < NPAIR - 2:
                    sqrt_rows(s - 4 - NPAIR2, slice(1, 2))
                if has_mx:
                    mx_bank(s - 3, 2)
                    mx_bank(s - 3, 3)
                else:
                    fill_warmth(s, 1)
                run_t(t_ops[12:24])
                if has_b:
                    exit_mx(s - 1, 1)
                    squares(s - 1, 0)
                if has_c:
                    reduce_h(s - 2)
                if NPAIR2 <= s - 3 < NPAIR - 1:
                    sqrt_rows(s - 3 - NPAIR2, slice(0, 1))
                if s in (NPAIR, NPAIR + 1):
                    first_turns_bits(s - NPAIR)
                if s % 2 == 1 and (s + 5) // 2 < NPAIR // 2:
                    load((s + 5) // 2)

        npv = ctx.enter_context(tc.tile_pool(name="npv", bufs=4))
        p_s = ctx.enter_context(tc.psum_pool(name="p_s", bufs=8))
        cos_tiles = {}

        def flat(u):
            return o_tiles[u].rearrange("p b j -> p (b j)")

        def turns_bits(k, h):
            nt = npv.tile([P, 2, N2], I32, name="ntb")
            nc.vector.tensor_scalar(
                out=nt[:], in0=quads[k][:, 2 * h : 2 * h + 2, :],
                scalar1=0.25 * UNIT, scalar2=NEG_BITS, op0=ALU.add, op1=ALU.add,
            )
            n_tiles.setdefault(k, []).append(nt)

        v_tiles = {}

        def turns(u):
            nt = npv.tile([P, 2 * N2], I32, name="ntv", bufs=2)
            nc.vector.tensor_scalar(
                out=nt[:], in0=flat(u), scalar1=0.25, scalar2=None, op0=ALU.add
            )
            v_tiles[u] = nt

        def subtract_turns(u):
            nc.vector.scalar_tensor_tensor(
                out=flat(u), in0=flat(u), scalar=0.25, in1=v_tiles[u][:],
                op0=ALU.add, op1=ALU.subtract,
            )

        def cos_tensor(k, half):
            if half == 0:
                cos_tiles[k] = obuf.tile(
                    [P, 8, 4 * P], F32, name="quad", bufs=NPAIR1 // 4 + 1
                )
            ct = cos_tiles[k]
            nf = n_tiles[k]
            for jp in (2 * half, 2 * half + 1):
                banks = [p_s.tile([P, 4, P], F32, name="ps") for i in range(2)]
                for ps in banks:
                    psf = ps[:].rearrange("p b r -> p (b r)")
                    nc.tensor.matmul(psf, lhsT=big[:, 0:P], rhs=big[:], start=True, stop=False)
                nc.tensor.matmul(
                    psf[:, 0:256], lhsT=big[:, 0:P], rhs=zero[:], start=False, stop=False
                )
                for i in range(2):
                    cols = slice(P * (2 * jp + i), P * (2 * jp + i) + P)
                    for rb in range(4):
                        for i_ap, last in (
                            (nf[rb // 2][:, rb % 2, cols].bitcast(F32), False),
                            (quads[k][:, rb, cols], rb == 3),
                        ):
                            nc.tensor.matmul(
                                banks[i][:, rb, :], lhsT=i_ap, rhs=identf[:],
                                is_transpose=True, start=False, stop=last,
                            )
                    nc.scalar.activation(
                        out=ct[:, 2 * jp + i, :],
                        in_=banks[i][:].rearrange("p b r -> p (b r)"),
                        func=ACT.Sin, scale=2.0 * PI / UNIT, bias=0.5 * PI,
                    )

        def cos_scalar(u):
            nc.scalar.activation(out=flat(u), in_=flat(u), func=ACT.Sin, scale=2.0 * PI)

        def spread_w():
            for half, pw in enumerate(spread(w_sb, p_s, "ps")):
                nc.vector.tensor_copy(
                    out=w2b[:, 512 * half : 512 * half + 512].rearrange(
                        "p (c n e) -> p c n e", c=2, e=2
                    ),
                    in_=pw[:].rearrange("p (c e) n -> p c n e", e=2),
                )

        def turn_w():
            for half in range(2):
                ps = p_s.tile([P, 4, P], F32, name="ps")
                for m in range(4):
                    cols = slice(P * (4 * half + m), P * (4 * half + m) + P)
                    nc.tensor.matmul(
                        ps[:, m, :], lhsT=w2b[:, cols], rhs=identf[:],
                        is_transpose=True, start=True, stop=True,
                    )
                nc.vector.tensor_copy(
                    out=w_nat[:, 4 * half : 4 * half + 4].rearrange("p (m o) -> p m o", o=1),
                    in_=ps[:, :, 0:1],
                )

        for k in range(NPAIR1 // 4):
            turns(4 * k + 2)
            if k + 1 < NPAIR1 // 4:
                turns_bits(k + 1, 0)
            else:
                turns(4 * k + 3)
            subtract_turns(4 * k + 2)
            if k + 1 < NPAIR1 // 4:
                turns(4 * k + 3)
                turns_bits(k + 1, 1)
            subtract_turns(4 * k + 3)
            cos_tensor(k, 0)
            if k == NPAIR1 // 4 - 1:
                spread_w()
            cos_scalar(4 * k + 2)
            cos_tensor(k, 1)
            cos_scalar(4 * k + 3)

        def scale_vector(u):
            nc.vector.scalar_tensor_tensor(
                out=o_tiles[u], in0=o_tiles[u], scalar=-1.0,
                in1=w2b[:].rearrange("p (o j) -> p o j", o=1).to_broadcast([P, 2, N2]),
                op0=ALU.add, op1=ALU.mult,
            )

        def scale_turned(k):
            ct = cos_tiles[k]
            for m in range(8):
                nc.vector.tensor_scalar(
                    out=ct[:, m, :], in0=ct[:, m, :], scalar1=-1.0, scalar2=w_nat[:, m : m + 1],
                    op0=ALU.add, op1=ALU.mult,
                )

        def exp_turned(k, last):
            ct = cos_tiles[k]
            ot = obuf.tile([P, 4, N2], F32, name="quad", bufs=NPAIR1 // 4 + 1)
            for rb in range(4):
                for half in range(2):
                    ps = p_s.tile([P, 4, P], F32, name="ps")
                    for m in range(4):
                        nc.tensor.matmul(
                            ps[:, m, :], lhsT=ct[:, 4 * half + m, P * rb : P * rb + P],
                            rhs=identf[:], is_transpose=True, start=True, stop=True,
                        )
                    cols = slice(512 * half, 512 * half + 512)
                    nc.scalar.activation(
                        out=ot[:, rb, cols], in_=ps[:].rearrange("p m r -> p (m r)"),
                        func=ACT.Exp,
                    )
                    if last and rb == 3:
                        nc.sync.dma_start(out=outv[:, 8 * k + 3, cols], in_=ot[:, 3, cols])
                if last and rb < 3:
                    nc.sync.dma_start(out=outv[:, 8 * k + rb, :], in_=ot[:, rb, :])
                elif not last and rb % 2 == 1:
                    nc.sync.dma_start(
                        out=outv[:, 8 * k + rb - 1 : 8 * k + rb + 1, :], in_=ot[:, rb - 1 : rb + 1, :]
                    )

        def exp_store(u, pieces):
            if pieces == 1:
                nc.scalar.activation(out=flat(u), in_=flat(u), func=ACT.Exp)
                nc.sync.dma_start(out=outv[:, 2 * u : 2 * u + 2, :], in_=o_tiles[u])
                return
            for b in range(2):
                for c in range(pieces // 2):
                    width = 2 * N2 // pieces
                    cols = slice(width * c, width * c + width)
                    piece = o_tiles[u][:, b, cols]
                    nc.scalar.activation(out=piece, in_=piece, func=ACT.Exp)
                    nc.sync.dma_start(out=outv[:, 2 * u + b, cols], in_=piece)

        for k in range(NPAIR1 // 4):
            last = k == NPAIR1 // 4 - 1
            scale_vector(4 * k + 2)
            if k == 0:
                turn_w()
            exp_store(4 * k + 2, 4 if k == 0 else 1)
            scale_vector(4 * k + 3)
            exp_store(4 * k + 3, 1)
            scale_turned(k)
            exp_turned(k, last)
